import numpy as np
import ml_dtypes


def mxq(x, axis, fmt="e4m3"):
    dtype, down = {"e4m3": (ml_dtypes.float8_e4m3fn, 7), "e5m2": (ml_dtypes.float8_e5m2, 14)}[fmt]
    v = np.moveaxis(np.asarray(x, np.float32).astype(ml_dtypes.bfloat16).astype(np.float64), axis, -1)
    blocks = v.reshape(v.shape[:-1] + (-1, 32))
    amax = np.abs(blocks).max(-1, keepdims=True)
    byte = np.maximum(np.where(amax > 0, np.frexp(amax)[1] - 1 + 127, 0) - down, 1)
    scale = np.exp2(byte - 127.0)
    codes = (blocks / scale).astype(np.float32).astype(dtype).astype(np.float64)
    return np.moveaxis((codes * scale).reshape(v.shape), -1, axis)


WIDE = False


def mx_kscale(k):
    if not WIDE:
        return np.ones(k)
    levels = np.array([10, -10, 5, -5, 0])
    a = np.random.permutation(np.resize(levels, k // 512 * 4)).reshape(k // 512, 4)
    idx = np.arange(k)
    return np.exp2(a[idx // 512, idx % 128 // 32])


BF16 = ml_dtypes.bfloat16


def bf(x):
    return np.asarray(x, np.float32).astype(BF16)


def f64(x):
    return np.asarray(x).astype(np.float64)


E2M1 = np.array([0.0, 0.5, 1.0, 1.5, 2.0, 3.0, 4.0, 6.0, -0.0, -0.5, -1.0, -1.5, -2.0, -3.0, -4.0, -6.0])


def pack_weight(w, fmt):
    k, n = w.shape
    w = f64(bf(w)).reshape(k // 32, 32, n)
    amax = np.abs(w).max(1)
    if fmt == "e4m3":
        byte = np.frexp(amax)[1] - 1 + 127 - 7
    else:
        mant, ex = np.frexp(amax / 6.0)
        byte = np.where(mant > 0.5, ex, ex - 1) + 127
    byte = np.clip(np.where(amax > 0, byte, 1), 1, 254)
    scaled = (w * np.exp2(127.0 - byte)[:, None, :]).reshape(k, n).astype(np.float32)
    by_word = np.ascontiguousarray(scaled.reshape(k // 512, 128, 4, n).transpose(0, 1, 3, 2))
    if fmt == "e4m3":
        words = by_word.astype(ml_dtypes.float8_e4m3fn).view(np.uint8)
    else:
        c = by_word.astype(ml_dtypes.float4_e2m1fn).view(np.uint8) & 0xF
        words = c[..., 0::2] | (c[..., 1::2] << 4)
    return np.ascontiguousarray(words), np.ascontiguousarray(byte.astype(np.uint8).reshape(k // 512, 16, n))


def unpack_weight(words, scales, fmt):
    g, p, n, _ = words.shape
    if fmt == "e4m3":
        vals = np.ascontiguousarray(words).view(ml_dtypes.float8_e4m3fn).astype(np.float64)
    else:
        nib = np.empty((g, p, n, 4), np.uint8)
        nib[..., 0::2] = words & 0xF
        nib[..., 1::2] = words >> 4
        vals = E2M1[nib]
    vals = vals * np.repeat(np.exp2(scales.astype(np.float64) - 127.0), 8, axis=1)[..., None]
    return vals.transpose(0, 1, 3, 2).reshape(g * 512, n)

def pack4(w):
    words, scales = pack_weight(w, "e2m1")
    return words.reshape(words.shape[0], 128, -1), scales


def unpack4(words, scales):
    return unpack_weight(words.reshape(words.shape[0], 128, -1, 2), scales, "e2m1")


S, HID, H, KV, D, WINDOW, QB = 1024, 1024, 8, 4, 256, 512, 512
NQ, NK = H * D, KV * D
EPS = 1e-6
ROPE_THETA = 10000.0


def rms_norm(x, w):
    var = np.mean(x * x, axis=-1, keepdims=True)
    return x * (1.0 / np.sqrt(var + EPS)) * (1.0 + w)


def rotate_half(x):
    x1, x2 = np.split(x, 2, axis=-1)
    return np.concatenate([-x2, x1], axis=-1)


def apply_rope(x, cos, sin):
    return x * cos[:, None, :] + rotate_half(x) * sin[:, None, :]


def setup_inputs():
    s = mx_kscale(HID)
    inv_freq = 1.0 / ROPE_THETA ** (np.arange(0, D, 2) / D)
    freqs = np.outer(np.arange(S), inv_freq)
    emb = np.concatenate([freqs, freqs], -1)
    hidden_states = bf(np.random.standard_normal((S, HID)) * s)
    words, scales = pack4(np.random.standard_normal((HID, NQ + NK + NK)) / np.sqrt(HID) / s[:, None])
    return {"hidden_states": hidden_states,
            "w_qkv_words": words, "w_qkv_scales": scales,
            "q_norm_w": bf(1.0 + 0.1 * np.random.standard_normal(D)),
            "k_norm_w": bf(1.0 + 0.1 * np.random.standard_normal(D)),
            "cos": bf(np.cos(emb)), "sin": bf(np.sin(emb))}


def reference(hidden_states, w_qkv_words, w_qkv_scales, q_norm_w, k_norm_w, cos, sin):
    qkv = mxq(f64(hidden_states), 1, "e4m3") @ unpack4(w_qkv_words, w_qkv_scales)
    q = qkv[:, :NQ].reshape(S, H, D)
    k = qkv[:, NQ:NQ + NK].reshape(S, KV, D)
    v = qkv[:, NQ + NK:].reshape(S, KV, D)
    q = rms_norm(q, f64(q_norm_w))
    k = rms_norm(k, f64(k_norm_w))
    q = apply_rope(q, f64(cos), f64(sin))
    k = apply_rope(k, f64(cos), f64(sin))
    return q, k, v

@@ -1,0 +1,223 @@
+from contextlib import ExitStack
+
+import concourse.mybir as mybir
+from concourse.masks import make_identity
+
+F32 = mybir.dt.float32
+BF16 = mybir.dt.bfloat16
+I32 = mybir.dt.int32
+U32 = mybir.dt.uint32
+U8 = mybir.dt.uint8
+FP8X4 = mybir.dt.float8_e4m3fn_x4
+FP4X4 = mybir.dt.float4_e2m1fn_x4
+ACT = mybir.ActivationFunctionType
+ALU = mybir.AluOpType
+
+P = 128
+S = 1024
+HID = 1024
+D = 256
+HALF = D // 2
+Q_HEADS = 8
+KV_HEADS = 4
+N_ALL = (Q_HEADS + 2 * KV_HEADS) * D
+EPS = 1e-6
+
+K_PASS = 512
+PASSES = HID // K_PASS
+ROW_TILES = S // P
+BANK = 512
+HEADS_PER_BANK = BANK // D
+GROUP_HEADS = 4
+GROUP = GROUP_HEADS * D
+BANKS_PER_GROUP = GROUP // BANK
+Q_TABLE = 0
+K_TABLE = 1
+STRAIGHT = 0
+CROSSED = 1
+
+FLOPS = 2 * S * HID * N_ALL
+
+
+def tile_gemmaattention_pa_kernel(
+    tc, hidden_states, w_qkv_words, w_qkv_scales, q_norm_w, k_norm_w, cos, sin, out_0, out_1, out_2
+):
+    nc = tc.nc
+
+    hidden_rows = hidden_states.rearrange("(p m) k -> p m k", m=ROW_TILES)
+    cos_rows = cos.rearrange("(p m) d -> p m d", m=ROW_TILES)
+    sin_rows = sin.rearrange("(p m) d -> p m d", m=ROW_TILES)
+    q_rows = out_0.rearrange("(p m) h d -> p m h d", m=ROW_TILES)
+    k_rows = out_1.rearrange("(p m) h d -> p m h d", m=ROW_TILES)
+    v_rows = out_2.rearrange("(p m) h d -> p m (h d)", m=ROW_TILES)
+    words_by_partition = w_qkv_words.rearrange("g p b -> p g b")
+
+    with ExitStack() as ctx:
+        keep = ctx.enter_context(tc.tile_pool(name="keep", bufs=1))
+        stage = ctx.enter_context(tc.tile_pool(name="stage", bufs=2))
+        small = ctx.enter_context(tc.tile_pool(name="small", bufs=6))
+        products = ctx.enter_context(tc.tile_pool(name="products", bufs=3))
+        results = ctx.enter_context(tc.tile_pool(name="results", bufs=4))
+        psum_keep = ctx.enter_context(tc.psum_pool(name="psum_keep", bufs=1))
+        psum_acc = ctx.enter_context(tc.psum_pool(name="psum_acc", bufs=6))
+
+        hidden_sb = keep.tile([P, ROW_TILES, HID], BF16)
+        cos_sb = keep.tile([P, ROW_TILES, D], BF16)
+        sin_sb = keep.tile([P, ROW_TILES, D], BF16)
+        w_words = keep.tile([P, PASSES, 2 * N_ALL], U8, align_bytes=64)
+        w_scales = keep.tile([P, PASSES, N_ALL], U8, align_bytes=64)
+        x_words = keep.tile([P, ROW_TILES, PASSES * P], U32, align_bytes=64)
+        x_scales = keep.tile([P, ROW_TILES, PASSES * P], U8, align_bytes=64)
+        tables = keep.tile([P, ROW_TILES, 2, 2, D], F32)
+        identity = keep.tile([P, P], F32)
+        ones = keep.tile([P, P], BF16)
+        norm_w_row = keep.tile([P, 2 * D], BF16)
+        eps = keep.tile([P, 1], F32)
+        warm = keep.tile([P, 1], F32)
+
+        nc.vector.memset(w_scales[:].bitcast(I32), 0)
+        nc.vector.memset(eps[:], EPS)
+        nc.vector.memset(ones[:], 1.0)
+        nc.vector.memset(norm_w_row[:], 0.0)
+        make_identity(nc, identity[:])
+        nc.scalar.activation(out=warm[:], in_=eps[:], func=ACT.Abs_reciprocal_sqrt)
+
+        nc.scalar.dma_start(out=norm_w_row[0:1, 0:D], in_=q_norm_w.unsqueeze(0))
+        nc.scalar.dma_start(out=norm_w_row[0:1, D : 2 * D], in_=k_norm_w.unsqueeze(0))
+
+        def load_rows(first, last):
+            nc.sync.dma_start(out=hidden_sb[:, first:last, :], in_=hidden_rows[:, first:last, :])
+
+        def load_cos_sin(first, last):
+            nc.sync.dma_start(out=cos_sb[:, first:last, :], in_=cos_rows[:, first:last, :])
+            nc.sync.dma_start(out=sin_sb[:, first:last, :], in_=sin_rows[:, first:last, :])
+
+        def load_scales():
+            for g in range(PASSES):
+                for low_q in range(2):
+                    for r in range(4):
+                        nc.sync.dma_start(
+                            out=w_scales[32 * low_q + r : P : 64, g, :].bitcast(I32),
+                            in_=w_qkv_scales[g, 4 * low_q + r : 16 : 8, :].bitcast(I32),
+                        )
+
+        def load_words(group):
+            some = slice(2 * GROUP * group, 2 * GROUP * (group + 1))
+            nc.sync.dma_start(
+                out=w_words[:, :, some].bitcast(I32), in_=words_by_partition[:, :, some].bitcast(I32)
+            )
+
+        load_rows(0, 1)
+        load_cos_sin(0, 4)
+        load_scales()
+        load_words(0)
+        load_words(1)
+        load_rows(1, 2)
+        load_words(2)
+        load_words(3)
+        load_cos_sin(4, 8)
+        load_rows(2, 4)
+        load_rows(4, 8)
+
+        norm_w_all = psum_keep.tile([P, 2, D], F32)
+        nc.tensor.matmul(
+            out=norm_w_all[:].rearrange("p t d -> p (t d)"), lhsT=ones[:], rhs=norm_w_row[:], start=True, stop=True
+        )
+
+        def quantise_rows(m):
+            pairs = hidden_sb[:, m, :].bitcast(F32)
+            turned = psum_keep.tile([P, PASSES, 2, P], F32)
+            for g in range(PASSES):
+                for u in range(2):
+                    nc.tensor.transpose(
+                        turned[:, g, u, :], pairs[:, 256 * g + u : 256 * (g + 1) : 2], identity[:]
+                    )
+            grouped = stage.tile([P, PASSES * P * 4], BF16, align_bytes=64)
+            nc.scalar.copy(
+                out=grouped[:].bitcast(F32).rearrange("p (g r u) -> p g r u", g=PASSES, u=2),
+                in_=turned[:].rearrange("p g u r -> p g r u"),
+            )
+            nc.vector.quantize_mx(out=x_words[:, m, :].bitcast(FP8X4), scales=x_scales[:, m, :], in_=grouped[:])
+
+        def build_tables(m):
+            def for_q_and_k(row_values):
+                return row_values.unsqueeze(1).to_broadcast([P, 2, row_values.shape[1]])
+
+            low, high = slice(0, HALF), slice(HALF, D)
+            for kind, columns, angles in (
+                (STRAIGHT, slice(0, D), cos_sb[:, m, :]),
+                (CROSSED, low, sin_sb[:, m, high]),
+                (CROSSED, high, sin_sb[:, m, low]),
+            ):
+                nc.vector.scalar_tensor_tensor(
+                    out=tables[:, m, :, kind, columns],
+                    in0=norm_w_all[:, :, columns],
+                    scalar=1.0,
+                    in1=for_q_and_k(angles),
+                    op0=ALU.add,
+                    op1=ALU.mult,
+                )
+
+        def multiply(m, bank):
+            acc = psum_acc.tile([P, BANK], F32)
+            for g in range(PASSES):
+                nc.tensor.matmul_mx(
+                    out=acc[:],
+                    lhsT=x_words[:, m, P * g : P * (g + 1)].bitcast(FP8X4),
+                    lhsT_scale=x_scales[:, m, P * g : P * (g + 1)],
+                    rhs=w_words[:, g, 2 * BANK * bank : 2 * BANK * (bank + 1)].bitcast(FP4X4),
+                    rhs_scale=w_scales[:, g, BANK * bank : BANK * (bank + 1)],
+                    start=(g == 0),
+                    stop=(g == PASSES - 1),
+                )
+            return acc
+
+        def norm_and_rope(m, group, which_table, destination):
+            both = products.tile([P, GROUP_HEADS, 2, D], F32)
+            for b in range(BANKS_PER_GROUP):
+                acc = multiply(m, BANKS_PER_GROUP * group + b)
+                sum_sq = small.tile([P, HEADS_PER_BANK], F32)
+                rstd = small.tile([P, HEADS_PER_BANK], F32)
+                for h in range(HEADS_PER_BANK):
+                    squares = stage.tile([P, D], BF16, bufs=4)
+                    nc.scalar.activation(
+                        out=squares[:], in_=acc[:, D * h : D * (h + 1)], func=ACT.Square, accum_out=sum_sq[:, h : h + 1]
+                    )
+                nc.scalar.activation(
+                    out=rstd[:], in_=sum_sq[:], func=ACT.Abs_reciprocal_sqrt, scale=1.0 / D, bias=eps[:]
+                )
+                for h in range(HEADS_PER_BANK):
+                    nc.vector.scalar_tensor_tensor(
+                        out=both[:, HEADS_PER_BANK * b + h, :, :],
+                        in0=acc[:, D * h : D * (h + 1)].unsqueeze(1).to_broadcast([P, 2, D]),
+                        scalar=rstd[:, h : h + 1],
+                        in1=tables[:, m, which_table, :, :],
+                        op0=ALU.mult,
+                        op1=ALU.mult,
+                    )
+            rotated = results.tile([P, GROUP_HEADS, D], F32)
+            nc.gpsimd.tensor_tensor(
+                out=rotated[:, :, 0:HALF], in0=both[:, :, STRAIGHT, 0:HALF], in1=both[:, :, CROSSED, HALF:D], op=ALU.subtract
+            )
+            nc.gpsimd.tensor_tensor(
+                out=rotated[:, :, HALF:D], in0=both[:, :, STRAIGHT, HALF:D], in1=both[:, :, CROSSED, 0:HALF], op=ALU.add
+            )
+            nc.sync.dma_start(out=destination, in_=rotated[:])
+
+        def copy_values(m, group):
+            values = results.tile([P, GROUP], F32)
+            for b in range(BANKS_PER_GROUP):
+                acc = multiply(m, BANKS_PER_GROUP * group + b)
+                nc.scalar.copy(out=values[:, BANK * b : BANK * (b + 1)], in_=acc[:])
+            nc.sync.dma_start(out=v_rows[:, m, :], in_=values[:])
+
+        quantise_rows(0)
+        build_tables(0)
+        for m in range(ROW_TILES):
+            if m + 1 < ROW_TILES:
+                quantise_rows(m + 1)
+                build_tables(m + 1)
+            norm_and_rope(m, 0, Q_TABLE, q_rows[:, m, 0:GROUP_HEADS, :])
+            norm_and_rope(m, 1, Q_TABLE, q_rows[:, m, GROUP_HEADS:Q_HEADS, :])
+            norm_and_rope(m, 2, K_TABLE, k_rows[:, m, :, :])
+            copy_values(m, 3)

@@ -18,6 +18,8 @@ S = 1024
 HID = 1024
 D = 256
 HALF = D // 2
+LOW = 0
+HIGH = 1
 Q_HEADS = 8
 KV_HEADS = 4
 N_ALL = (Q_HEADS + 2 * KV_HEADS) * D
@@ -31,10 +33,13 @@ HEADS_PER_BANK = BANK // D
 GROUP_HEADS = 4
 GROUP = GROUP_HEADS * D
 BANKS_PER_GROUP = GROUP // BANK
+Q_LOW_GROUP = 0
+Q_HIGH_GROUP = 1
+K_GROUP = 2
+V_GROUP = 3
 Q_TABLE = 0
 K_TABLE = 1
-STRAIGHT = 0
-CROSSED = 1
+CHUNKS = ((0, 1), (1, 2), (2, 4), (4, 8))
 
 FLOPS = 2 * S * HID * N_ALL
 
@@ -56,7 +61,7 @@ def tile_gemmaattention_pa_kernel(
         keep = ctx.enter_context(tc.tile_pool(name="keep", bufs=1))
         stage = ctx.enter_context(tc.tile_pool(name="stage", bufs=2))
         small = ctx.enter_context(tc.tile_pool(name="small", bufs=6))
-        products = ctx.enter_context(tc.tile_pool(name="products", bufs=3))
+        work = ctx.enter_context(tc.tile_pool(name="work", bufs=3))
         results = ctx.enter_context(tc.tile_pool(name="results", bufs=4))
         psum_keep = ctx.enter_context(tc.psum_pool(name="psum_keep", bufs=1))
         psum_acc = ctx.enter_context(tc.psum_pool(name="psum_acc", bufs=6))
@@ -64,26 +69,28 @@ def tile_gemmaattention_pa_kernel(
         hidden_sb = keep.tile([P, ROW_TILES, HID], BF16)
         cos_sb = keep.tile([P, ROW_TILES, D], BF16)
         sin_sb = keep.tile([P, ROW_TILES, D], BF16)
+        minus_sin_low = keep.tile([P, ROW_TILES, HALF], BF16)
         w_words = keep.tile([P, PASSES, 2 * N_ALL], U8, align_bytes=64)
         w_scales = keep.tile([P, PASSES, N_ALL], U8, align_bytes=64)
         x_words = keep.tile([P, ROW_TILES, PASSES * P], U32, align_bytes=64)
         x_scales = keep.tile([P, ROW_TILES, PASSES * P], U8, align_bytes=64)
-        tables = keep.tile([P, ROW_TILES, 2, 2, D], F32)
+        tables = keep.tile([P, ROW_TILES, 2, 2, 2, HALF], F32)
         identity = keep.tile([P, P], F32)
         ones = keep.tile([P, P], BF16)
-        norm_w_row = keep.tile([P, 2 * D], BF16)
+        norm_w_rows = keep.tile([P, 2 * D], BF16)
         eps = keep.tile([P, 1], F32)
         warm = keep.tile([P, 1], F32)
 
+        nc.vector.memset(norm_w_rows[:], 0.0)
+        nc.vector.memset(norm_w_rows[32:33, :], 1.0)
         nc.vector.memset(w_scales[:].bitcast(I32), 0)
         nc.vector.memset(eps[:], EPS)
         nc.vector.memset(ones[:], 1.0)
-        nc.vector.memset(norm_w_row[:], 0.0)
         make_identity(nc, identity[:])
         nc.scalar.activation(out=warm[:], in_=eps[:], func=ACT.Abs_reciprocal_sqrt)
 
-        nc.scalar.dma_start(out=norm_w_row[0:1, 0:D], in_=q_norm_w.unsqueeze(0))
-        nc.scalar.dma_start(out=norm_w_row[0:1, D : 2 * D], in_=k_norm_w.unsqueeze(0))
+        nc.sync.dma_start(out=norm_w_rows[0:1, 0:D], in_=q_norm_w.unsqueeze(0))
+        nc.sync.dma_start(out=norm_w_rows[0:1, D : 2 * D], in_=k_norm_w.unsqueeze(0))
 
         def load_rows(first, last):
             nc.sync.dma_start(out=hidden_sb[:, first:last, :], in_=hidden_rows[:, first:last, :])
@@ -91,15 +98,16 @@ def tile_gemmaattention_pa_kernel(
         def load_cos_sin(first, last):
             nc.sync.dma_start(out=cos_sb[:, first:last, :], in_=cos_rows[:, first:last, :])
             nc.sync.dma_start(out=sin_sb[:, first:last, :], in_=sin_rows[:, first:last, :])
+            nc.vector.tensor_scalar_mul(
+                out=minus_sin_low[:, first:last, :], in0=sin_sb[:, first:last, 0:HALF], scalar1=-1.0
+            )
 
         def load_scales():
-            for g in range(PASSES):
-                for low_q in range(2):
-                    for r in range(4):
-                        nc.sync.dma_start(
-                            out=w_scales[32 * low_q + r : P : 64, g, :].bitcast(I32),
-                            in_=w_qkv_scales[g, 4 * low_q + r : 16 : 8, :].bitcast(I32),
-                        )
+            for r in range(4):
+                nc.sync.dma_start(
+                    out=w_scales[r : P : 32, :, :].bitcast(I32),
+                    in_=w_qkv_scales[:, r : 16 : 4, :].rearrange("g q n -> q g n").bitcast(I32),
+                )
 
         def load_words(group):
             some = slice(2 * GROUP * group, 2 * GROUP * (group + 1))
@@ -108,55 +116,58 @@ def tile_gemmaattention_pa_kernel(
             )
 
         load_rows(0, 1)
-        load_cos_sin(0, 4)
         load_scales()
-        load_words(0)
-        load_words(1)
+        load_words(Q_LOW_GROUP)
+        load_cos_sin(0, 4)
+        load_words(Q_HIGH_GROUP)
         load_rows(1, 2)
-        load_words(2)
-        load_words(3)
-        load_cos_sin(4, 8)
+        load_words(V_GROUP)
+        load_words(K_GROUP)
         load_rows(2, 4)
+        load_cos_sin(4, 8)
         load_rows(4, 8)
 
-        norm_w_all = psum_keep.tile([P, 2, D], F32)
+        gain = psum_keep.tile([P, 2, 2, HALF], F32)
         nc.tensor.matmul(
-            out=norm_w_all[:].rearrange("p t d -> p (t d)"), lhsT=ones[:], rhs=norm_w_row[:], start=True, stop=True
+            out=gain[:].rearrange("p t h d -> p (t h d)"), lhsT=ones[:], rhs=norm_w_rows[:], start=True, stop=True
         )
 
-        def quantise_rows(m):
-            pairs = hidden_sb[:, m, :].bitcast(F32)
-            turned = psum_keep.tile([P, PASSES, 2, P], F32)
-            for g in range(PASSES):
-                for u in range(2):
-                    nc.tensor.transpose(
-                        turned[:, g, u, :], pairs[:, 256 * g + u : 256 * (g + 1) : 2], identity[:]
-                    )
-            grouped = stage.tile([P, PASSES * P * 4], BF16, align_bytes=64)
-            nc.scalar.copy(
-                out=grouped[:].bitcast(F32).rearrange("p (g r u) -> p g r u", g=PASSES, u=2),
-                in_=turned[:].rearrange("p g u r -> p g r u"),
-            )
-            nc.vector.quantize_mx(out=x_words[:, m, :].bitcast(FP8X4), scales=x_scales[:, m, :], in_=grouped[:])
-
-        def build_tables(m):
-            def for_q_and_k(row_values):
-                return row_values.unsqueeze(1).to_broadcast([P, 2, row_values.shape[1]])
-
-            low, high = slice(0, HALF), slice(HALF, D)
-            for kind, columns, angles in (
-                (STRAIGHT, slice(0, D), cos_sb[:, m, :]),
-                (CROSSED, low, sin_sb[:, m, high]),
-                (CROSSED, high, sin_sb[:, m, low]),
-            ):
-                nc.vector.scalar_tensor_tensor(
-                    out=tables[:, m, :, kind, columns],
-                    in0=norm_w_all[:, :, columns],
-                    scalar=1.0,
-                    in1=for_q_and_k(angles),
-                    op0=ALU.add,
-                    op1=ALU.mult,
+        def quantise_rows(first, last):
+            grouped = stage.tile([P, last - first, PASSES * P * 4], BF16, align_bytes=64, tag="grouped")
+            for m in range(first, last):
+                pairs = hidden_sb[:, m, :].bitcast(F32)
+                turned = psum_keep.tile([P, PASSES, 2, P], F32)
+                for g in range(PASSES):
+                    for u in range(2):
+                        nc.tensor.transpose(
+                            turned[:, g, u, :], pairs[:, 256 * g + u : 256 * (g + 1) : 2], identity[:]
+                        )
+                nc.scalar.copy(
+                    out=grouped[:, m - first, :].bitcast(F32).rearrange("p (g r u) -> p g r u", g=PASSES, u=2),
+                    in_=turned[:].rearrange("p g u r -> p g r u"),
                 )
+            nc.vector.quantize_mx(
+                out=x_words[:, first:last, :].rearrange("p m c -> p (m c)").bitcast(FP8X4),
+                scales=x_scales[:, first:last, :].rearrange("p m c -> p (m c)"),
+                in_=grouped[:].rearrange("p m c -> p (m c)"),
+            )
+
+        def build_tables(first, last):
+            count = last - first
+            angle = {
+                (LOW, LOW): cos_sb[:, first:last, 0:HALF],
+                (LOW, HIGH): minus_sin_low[:, first:last, :],
+                (HIGH, LOW): sin_sb[:, first:last, HALF:D],
+                (HIGH, HIGH): cos_sb[:, first:last, HALF:D],
+            }
+            for target in (LOW, HIGH):
+                for source in (LOW, HIGH):
+                    nc.vector.tensor_tensor(
+                        out=tables[:, first:last, :, target, source, :],
+                        in0=gain[:, :, source, :].unsqueeze(1).to_broadcast([P, count, 2, HALF]),
+                        in1=angle[(target, source)].unsqueeze(2).to_broadcast([P, count, 2, HALF]),
+                        op=ALU.mult,
+                    )
 
         def multiply(m, bank):
             acc = psum_acc.tile([P, BANK], F32)
@@ -172,8 +183,8 @@ def tile_gemmaattention_pa_kernel(
                 )
             return acc
 
-        def norm_and_rope(m, group, which_table, destination):
-            both = products.tile([P, GROUP_HEADS, 2, D], F32)
+        def norm_and_rope(m, group, which_table, adder, destination):
+            products = work.tile([P, GROUP_HEADS, 2, 2, HALF], F32)
             for b in range(BANKS_PER_GROUP):
                 acc = multiply(m, BANKS_PER_GROUP * group + b)
                 sum_sq = small.tile([P, HEADS_PER_BANK], F32)
@@ -188,36 +199,37 @@ def tile_gemmaattention_pa_kernel(
                 )
                 for h in range(HEADS_PER_BANK):
                     nc.vector.scalar_tensor_tensor(
-                        out=both[:, HEADS_PER_BANK * b + h, :, :],
+                        out=products[:, HEADS_PER_BANK * b + h].rearrange("p t s d -> p t (s d)"),
                         in0=acc[:, D * h : D * (h + 1)].unsqueeze(1).to_broadcast([P, 2, D]),
                         scalar=rstd[:, h : h + 1],
-                        in1=tables[:, m, which_table, :, :],
+                        in1=tables[:, m, which_table].rearrange("p t s d -> p t (s d)"),
                         op0=ALU.mult,
                         op1=ALU.mult,
                     )
-            rotated = results.tile([P, GROUP_HEADS, D], F32)
-            nc.gpsimd.tensor_tensor(
-                out=rotated[:, :, 0:HALF], in0=both[:, :, STRAIGHT, 0:HALF], in1=both[:, :, CROSSED, HALF:D], op=ALU.subtract
+            rotated = results.tile([P, GROUP_HEADS, 2, HALF], F32)
+            adder.tensor_tensor(
+                out=rotated[:], in0=products[:, :, :, LOW, :], in1=products[:, :, :, HIGH, :], op=ALU.add
             )
-            nc.gpsimd.tensor_tensor(
-                out=rotated[:, :, HALF:D], in0=both[:, :, STRAIGHT, HALF:D], in1=both[:, :, CROSSED, 0:HALF], op=ALU.add
-            )
-            nc.sync.dma_start(out=destination, in_=rotated[:])
+            nc.sync.dma_start(out=destination, in_=rotated[:].rearrange("p h t d -> p h (t d)"))
 
-        def copy_values(m, group):
+        def copy_values(m):
             values = results.tile([P, GROUP], F32)
             for b in range(BANKS_PER_GROUP):
-                acc = multiply(m, BANKS_PER_GROUP * group + b)
+                acc = multiply(m, BANKS_PER_GROUP * V_GROUP + b)
                 nc.scalar.copy(out=values[:, BANK * b : BANK * (b + 1)], in_=acc[:])
             nc.sync.dma_start(out=v_rows[:, m, :], in_=values[:])
 
-        quantise_rows(0)
-        build_tables(0)
-        for m in range(ROW_TILES):
-            if m + 1 < ROW_TILES:
-                quantise_rows(m + 1)
-                build_tables(m + 1)
-            norm_and_rope(m, 0, Q_TABLE, q_rows[:, m, 0:GROUP_HEADS, :])
-            norm_and_rope(m, 1, Q_TABLE, q_rows[:, m, GROUP_HEADS:Q_HEADS, :])
-            norm_and_rope(m, 2, K_TABLE, k_rows[:, m, :, :])
-            copy_values(m, 3)
+        def prepare(chunk):
+            quantise_rows(chunk[0], chunk[1])
+            build_tables(chunk[0], chunk[1])
+
+        prepare(CHUNKS[0])
+        for c in range(len(CHUNKS)):
+            if c + 1 < len(CHUNKS):
+                prepare(CHUNKS[c + 1])
+            for m in range(CHUNKS[c][0], CHUNKS[c][1]):
+                norm_and_rope(m, Q_LOW_GROUP, Q_TABLE, nc.gpsimd, q_rows[:, m, 0:GROUP_HEADS, :])
+                norm_and_rope(m, Q_HIGH_GROUP, Q_TABLE, nc.gpsimd, q_rows[:, m, GROUP_HEADS:Q_HEADS, :])
+                copy_values(m)
+                last_adder = nc.vector if m == ROW_TILES - 1 else nc.gpsimd
+                norm_and_rope(m, K_GROUP, K_TABLE, last_adder, k_rows[:, m, :, :])

@@ -95,12 +95,10 @@ def tile_gemmaattention_pa_kernel(
         def load_rows(first, last):
             nc.sync.dma_start(out=hidden_sb[:, first:last, :], in_=hidden_rows[:, first:last, :])
 
-        def load_cos_sin(first, last):
-            nc.sync.dma_start(out=cos_sb[:, first:last, :], in_=cos_rows[:, first:last, :])
-            nc.sync.dma_start(out=sin_sb[:, first:last, :], in_=sin_rows[:, first:last, :])
-            nc.vector.tensor_scalar_mul(
-                out=minus_sin_low[:, first:last, :], in0=sin_sb[:, first:last, 0:HALF], scalar1=-1.0
-            )
+        def load_cos_sin():
+            nc.sync.dma_start(out=cos_sb[:], in_=cos_rows)
+            nc.sync.dma_start(out=sin_sb[:], in_=sin_rows)
+            nc.vector.tensor_scalar_mul(out=minus_sin_low[:], in0=sin_sb[:, :, 0:HALF], scalar1=-1.0)
 
         def load_scales():
             for r in range(4):
@@ -118,19 +116,20 @@ def tile_gemmaattention_pa_kernel(
         load_rows(0, 1)
         load_scales()
         load_words(Q_LOW_GROUP)
-        load_cos_sin(0, 4)
+        load_cos_sin()
         load_words(Q_HIGH_GROUP)
         load_rows(1, 2)
         load_words(V_GROUP)
         load_words(K_GROUP)
         load_rows(2, 4)
-        load_cos_sin(4, 8)
         load_rows(4, 8)
 
         gain = psum_keep.tile([P, 2, 2, HALF], F32)
         nc.tensor.matmul(
             out=gain[:].rearrange("p t h d -> p (t h d)"), lhsT=ones[:], rhs=norm_w_rows[:], start=True, stop=True
         )
+        gain_sb = keep.tile([P, 2, 2, HALF], F32)
+        nc.scalar.copy(out=gain_sb[:], in_=gain[:])
 
         def quantise_rows(first, last):
             grouped = stage.tile([P, last - first, PASSES * P * 4], BF16, align_bytes=64, tag="grouped")
@@ -152,7 +151,7 @@ def tile_gemmaattention_pa_kernel(
                 in_=grouped[:].rearrange("p m c -> p (m c)"),
             )
 
-        def build_tables(first, last):
+        def build_tables(engine, gain_values, first, last):
             count = last - first
             angle = {
                 (LOW, LOW): cos_sb[:, first:last, 0:HALF],
@@ -162,9 +161,9 @@ def tile_gemmaattention_pa_kernel(
             }
             for target in (LOW, HIGH):
                 for source in (LOW, HIGH):
-                    nc.vector.tensor_tensor(
+                    engine.tensor_tensor(
                         out=tables[:, first:last, :, target, source, :],
-                        in0=gain[:, :, source, :].unsqueeze(1).to_broadcast([P, count, 2, HALF]),
+                        in0=gain_values[:, :, source, :].unsqueeze(1).to_broadcast([P, count, 2, HALF]),
                         in1=angle[(target, source)].unsqueeze(2).to_broadcast([P, count, 2, HALF]),
                         op=ALU.mult,
                     )
@@ -221,15 +220,17 @@ def tile_gemmaattention_pa_kernel(
 
         def prepare(chunk):
             quantise_rows(chunk[0], chunk[1])
-            build_tables(chunk[0], chunk[1])
+            if chunk != CHUNKS[-1]:
+                build_tables(nc.vector, gain, chunk[0], chunk[1])
 
         prepare(CHUNKS[0])
+        build_tables(nc.gpsimd, gain_sb, CHUNKS[-1][0], CHUNKS[-1][1])
         for c in range(len(CHUNKS)):
             if c + 1 < len(CHUNKS):
                 prepare(CHUNKS[c + 1])
             for m in range(CHUNKS[c][0], CHUNKS[c][1]):
-                norm_and_rope(m, Q_LOW_GROUP, Q_TABLE, nc.gpsimd, q_rows[:, m, 0:GROUP_HEADS, :])
-                norm_and_rope(m, Q_HIGH_GROUP, Q_TABLE, nc.gpsimd, q_rows[:, m, GROUP_HEADS:Q_HEADS, :])
+                adder = nc.vector if m == ROW_TILES - 1 else nc.gpsimd
+                norm_and_rope(m, Q_LOW_GROUP, Q_TABLE, adder, q_rows[:, m, 0:GROUP_HEADS, :])
+                norm_and_rope(m, Q_HIGH_GROUP, Q_TABLE, adder, q_rows[:, m, GROUP_HEADS:Q_HEADS, :])
                 copy_values(m)
-                last_adder = nc.vector if m == ROW_TILES - 1 else nc.gpsimd
-                norm_and_rope(m, K_GROUP, K_TABLE, last_adder, k_rows[:, m, :, :])
+                norm_and_rope(m, K_GROUP, K_TABLE, adder, k_rows[:, m, :, :])

@@ -61,7 +61,7 @@ def tile_gemmaattention_pa_kernel(
         keep = ctx.enter_context(tc.tile_pool(name="keep", bufs=1))
         stage = ctx.enter_context(tc.tile_pool(name="stage", bufs=2))
         small = ctx.enter_context(tc.tile_pool(name="small", bufs=6))
-        work = ctx.enter_context(tc.tile_pool(name="work", bufs=3))
+        work = ctx.enter_context(tc.tile_pool(name="work", bufs=6))
         results = ctx.enter_context(tc.tile_pool(name="results", bufs=4))
         psum_keep = ctx.enter_context(tc.psum_pool(name="psum_keep", bufs=1))
         psum_acc = ctx.enter_context(tc.psum_pool(name="psum_acc", bufs=6))
@@ -182,8 +182,9 @@ def tile_gemmaattention_pa_kernel(
                 )
             return acc
 
-        def norm_and_rope(m, group, which_table, adder, destination):
+        def norm_and_rope(m, group, which_table, adder, pieces, destination):
             products = work.tile([P, GROUP_HEADS, 2, 2, HALF], F32)
+            rotated = results.tile([P, GROUP_HEADS, 2, HALF], F32)
             for b in range(BANKS_PER_GROUP):
                 acc = multiply(m, BANKS_PER_GROUP * group + b)
                 sum_sq = small.tile([P, HEADS_PER_BANK], F32)
@@ -205,11 +206,14 @@ def tile_gemmaattention_pa_kernel(
                         op0=ALU.mult,
                         op1=ALU.mult,
                     )
-            rotated = results.tile([P, GROUP_HEADS, 2, HALF], F32)
-            adder.tensor_tensor(
-                out=rotated[:], in0=products[:, :, :, LOW, :], in1=products[:, :, :, HIGH, :], op=ALU.add
-            )
-            nc.sync.dma_start(out=destination, in_=rotated[:].rearrange("p h t d -> p h (t d)"))
+                if (b + 1) % (BANKS_PER_GROUP // pieces) == 0:
+                    some = slice(HEADS_PER_BANK * (b + 1) - GROUP_HEADS // pieces, HEADS_PER_BANK * (b + 1))
+                    adder.tensor_tensor(
+                        out=rotated[:, some], in0=products[:, some, :, LOW, :], in1=products[:, some, :, HIGH, :], op=ALU.add
+                    )
+                    nc.sync.dma_start(
+                        out=destination[:, some, :], in_=rotated[:, some].rearrange("p h t d -> p h (t d)")
+                    )
 
         def copy_values(m):
             values = results.tile([P, GROUP], F32)
@@ -229,8 +233,9 @@ def tile_gemmaattention_pa_kernel(
             if c + 1 < len(CHUNKS):
                 prepare(CHUNKS[c + 1])
             for m in range(CHUNKS[c][0], CHUNKS[c][1]):
-                adder = nc.vector if m == ROW_TILES - 1 else nc.gpsimd
-                norm_and_rope(m, Q_LOW_GROUP, Q_TABLE, adder, q_rows[:, m, 0:GROUP_HEADS, :])
-                norm_and_rope(m, Q_HIGH_GROUP, Q_TABLE, adder, q_rows[:, m, GROUP_HEADS:Q_HEADS, :])
+                late_adder = nc.vector if m == ROW_TILES - 1 else nc.gpsimd
+                last_pieces = BANKS_PER_GROUP if m == ROW_TILES - 1 else 1
+                norm_and_rope(m, Q_LOW_GROUP, Q_TABLE, nc.gpsimd, 1, q_rows[:, m, 0:GROUP_HEADS, :])
+                norm_and_rope(m, Q_HIGH_GROUP, Q_TABLE, late_adder, 1, q_rows[:, m, GROUP_HEADS:Q_HEADS, :])
                 copy_values(m)
-                norm_and_rope(m, K_GROUP, K_TABLE, adder, k_rows[:, m, :, :])
+                norm_and_rope(m, K_GROUP, K_TABLE, late_adder, last_pieces, k_rows[:, m, :, :])

@@ -40,6 +40,7 @@ V_GROUP = 3
 Q_TABLE = 0
 K_TABLE = 1
 CHUNKS = ((0, 1), (1, 2), (2, 4), (4, 8))
+GPSIMD_TABLES_FROM = 4
 
 FLOPS = 2 * S * HID * N_ALL
 
@@ -83,28 +84,34 @@ def tile_gemmaattention_pa_kernel(
 
         nc.vector.memset(norm_w_rows[:], 0.0)
         nc.vector.memset(norm_w_rows[32:33, :], 1.0)
-        nc.vector.memset(w_scales[:].bitcast(I32), 0)
-        nc.vector.memset(eps[:], EPS)
         nc.vector.memset(ones[:], 1.0)
+        nc.vector.memset(eps[:], EPS)
+
+        def zero_scales(first, last):
+            nc.vector.memset(w_scales[:, :, first:last].bitcast(I32), 0)
+
+        zero_scales(0, GROUP)
+        zero_scales(GROUP, N_ALL)
         make_identity(nc, identity[:])
         nc.scalar.activation(out=warm[:], in_=eps[:], func=ACT.Abs_reciprocal_sqrt)
-
-        nc.sync.dma_start(out=norm_w_rows[0:1, 0:D], in_=q_norm_w.unsqueeze(0))
-        nc.sync.dma_start(out=norm_w_rows[0:1, D : 2 * D], in_=k_norm_w.unsqueeze(0))
 
         def load_rows(first, last):
             nc.sync.dma_start(out=hidden_sb[:, first:last, :], in_=hidden_rows[:, first:last, :])
 
-        def load_cos_sin():
-            nc.sync.dma_start(out=cos_sb[:], in_=cos_rows)
-            nc.sync.dma_start(out=sin_sb[:], in_=sin_rows)
-            nc.vector.tensor_scalar_mul(out=minus_sin_low[:], in0=sin_sb[:, :, 0:HALF], scalar1=-1.0)
+        def load_cos(first, last):
+            nc.sync.dma_start(out=cos_sb[:, first:last, :], in_=cos_rows[:, first:last, :])
 
-        def load_scales():
+        def load_sin(first, last):
+            nc.sync.dma_start(out=sin_sb[:, first:last, :], in_=sin_rows[:, first:last, :])
+            nc.vector.tensor_scalar_mul(
+                out=minus_sin_low[:, first:last, :], in0=sin_sb[:, first:last, 0:HALF], scalar1=-1.0
+            )
+
+        def load_scales(first, last):
             for r in range(4):
                 nc.sync.dma_start(
-                    out=w_scales[r : P : 32, :, :].bitcast(I32),
-                    in_=w_qkv_scales[:, r : 16 : 4, :].rearrange("g q n -> q g n").bitcast(I32),
+                    out=w_scales[r : P : 32, :, first:last].bitcast(I32),
+                    in_=w_qkv_scales[:, r : 16 : 4, first:last].rearrange("g q n -> q g n").bitcast(I32),
                 )
 
         def load_words(group):
@@ -113,12 +120,18 @@ def tile_gemmaattention_pa_kernel(
                 out=w_words[:, :, some].bitcast(I32), in_=words_by_partition[:, :, some].bitcast(I32)
             )
 
+        load_cos(0, 4)
+        nc.sync.dma_start(out=norm_w_rows[0:1, 0:D], in_=q_norm_w.unsqueeze(0))
+        nc.sync.dma_start(out=norm_w_rows[0:1, D : 2 * D], in_=k_norm_w.unsqueeze(0))
+        load_sin(0, 4)
+        load_cos(4, 8)
+        load_sin(4, 8)
         load_rows(0, 1)
-        load_scales()
+        load_scales(0, GROUP)
         load_words(Q_LOW_GROUP)
-        load_cos_sin()
         load_words(Q_HIGH_GROUP)
         load_rows(1, 2)
+        load_scales(GROUP, N_ALL)
         load_words(V_GROUP)
         load_words(K_GROUP)
         load_rows(2, 4)
@@ -224,11 +237,11 @@ def tile_gemmaattention_pa_kernel(
 
         def prepare(chunk):
             quantise_rows(chunk[0], chunk[1])
-            if chunk != CHUNKS[-1]:
-                build_tables(nc.vector, gain, chunk[0], chunk[1])
+            if chunk[0] < GPSIMD_TABLES_FROM:
+                build_tables(nc.vector, gain, chunk[0], min(chunk[1], GPSIMD_TABLES_FROM))
 
         prepare(CHUNKS[0])
-        build_tables(nc.gpsimd, gain_sb, CHUNKS[-1][0], CHUNKS[-1][1])
+        build_tables(nc.gpsimd, gain_sb, GPSIMD_TABLES_FROM, ROW_TILES)
         for c in range(len(CHUNKS)):
             if c + 1 < len(CHUNKS):
                 prepare(CHUNKS[c + 1])

@@ -40,7 +40,15 @@ V_GROUP = 3
 Q_TABLE = 0
 K_TABLE = 1
 CHUNKS = ((0, 1), (1, 2), (2, 4), (4, 8))
-GPSIMD_TABLES_FROM = 4
+VECTOR_TABLES_TO = 2
+GPSIMD_TABLES_TO = 4
+TABLE_LEAD = 2
+VECTOR_LAST_ADDS = 1
+PLUS_ONE = 0
+MINUS_ONE = 1
+TIMES_W = 2
+MINUS_W_HIGH = 4
+ANGLE_PLACE = ((0, 1), (2, 3))
 
 FLOPS = 2 * S * HID * N_ALL
 
@@ -70,13 +78,15 @@ def tile_gemmaattention_pa_kernel(
         hidden_sb = keep.tile([P, ROW_TILES, HID], BF16)
         cos_sb = keep.tile([P, ROW_TILES, D], BF16)
         sin_sb = keep.tile([P, ROW_TILES, D], BF16)
-        minus_sin_low = keep.tile([P, ROW_TILES, HALF], BF16)
         w_words = keep.tile([P, PASSES, 2 * N_ALL], U8, align_bytes=64)
         w_scales = keep.tile([P, PASSES, N_ALL], U8, align_bytes=64)
         x_words = keep.tile([P, ROW_TILES, PASSES * P], U32, align_bytes=64)
         x_scales = keep.tile([P, ROW_TILES, PASSES * P], U8, align_bytes=64)
         tables = keep.tile([P, ROW_TILES, 2, 2, 2, HALF], F32)
         identity = keep.tile([P, P], F32)
+        identity_bf = keep.tile([P, P], BF16)
+        first_row = keep.tile([P, P], BF16)
+        scalers = keep.tile([P, 5, 2, HALF], BF16)
         ones = keep.tile([P, P], BF16)
         norm_w_rows = keep.tile([P, 2 * D], BF16)
         eps = keep.tile([P, 1], F32)
@@ -85,6 +95,8 @@ def tile_gemmaattention_pa_kernel(
         nc.vector.memset(norm_w_rows[:], 0.0)
         nc.vector.memset(norm_w_rows[32:33, :], 1.0)
         nc.vector.memset(ones[:], 1.0)
+        nc.vector.memset(first_row[:], 0.0)
+        nc.vector.memset(first_row[0:1, :], 1.0)
         nc.vector.memset(eps[:], EPS)
 
         def zero_scales(first, last):
@@ -93,6 +105,16 @@ def tile_gemmaattention_pa_kernel(
         zero_scales(0, GROUP)
         zero_scales(GROUP, N_ALL)
         make_identity(nc, identity[:])
+        make_identity(nc, identity_bf[:])
+        for place, sign in ((PLUS_ONE, 1.0), (MINUS_ONE, -1.0)):
+            nc.gpsimd.tensor_scalar(
+                out=scalers[:, place],
+                in0=identity[:].unsqueeze(1).to_broadcast([P, 2, HALF]),
+                scalar1=sign,
+                scalar2=0.0,
+                op0=ALU.mult,
+                op1=ALU.add,
+            )
         nc.scalar.activation(out=warm[:], in_=eps[:], func=ACT.Abs_reciprocal_sqrt)
 
         def load_rows(first, last):
@@ -103,9 +125,6 @@ def tile_gemmaattention_pa_kernel(
 
         def load_sin(first, last):
             nc.sync.dma_start(out=sin_sb[:, first:last, :], in_=sin_rows[:, first:last, :])
-            nc.vector.tensor_scalar_mul(
-                out=minus_sin_low[:, first:last, :], in0=sin_sb[:, first:last, 0:HALF], scalar1=-1.0
-            )
 
         def load_scales(first, last):
             for r in range(4):
@@ -120,13 +139,11 @@ def tile_gemmaattention_pa_kernel(
                 out=w_words[:, :, some].bitcast(I32), in_=words_by_partition[:, :, some].bitcast(I32)
             )
 
-        load_cos(0, 4)
         nc.sync.dma_start(out=norm_w_rows[0:1, 0:D], in_=q_norm_w.unsqueeze(0))
         nc.sync.dma_start(out=norm_w_rows[0:1, D : 2 * D], in_=k_norm_w.unsqueeze(0))
-        load_sin(0, 4)
-        load_cos(4, 8)
-        load_sin(4, 8)
         load_rows(0, 1)
+        load_cos(0, GPSIMD_TABLES_TO)
+        load_sin(0, GPSIMD_TABLES_TO)
         load_scales(0, GROUP)
         load_words(Q_LOW_GROUP)
         load_words(Q_HIGH_GROUP)
@@ -135,14 +152,72 @@ def tile_gemmaattention_pa_kernel(
         load_words(V_GROUP)
         load_words(K_GROUP)
         load_rows(2, 4)
+        load_cos(GPSIMD_TABLES_TO, ROW_TILES)
+        load_sin(GPSIMD_TABLES_TO, ROW_TILES)
         load_rows(4, 8)
 
-        gain = psum_keep.tile([P, 2, 2, HALF], F32)
+        gain = psum_keep.tile([P, 2, 2, HALF], F32, tag="spare")
         nc.tensor.matmul(
             out=gain[:].rearrange("p t h d -> p (t h d)"), lhsT=ones[:], rhs=norm_w_rows[:], start=True, stop=True
         )
-        gain_sb = keep.tile([P, 2, 2, HALF], F32)
-        nc.scalar.copy(out=gain_sb[:], in_=gain[:])
+        gain_sb = keep.tile([P, 2, 3, HALF], F32)
+        nc.scalar.copy(out=gain_sb[:, :, 0:2, :], in_=gain[:])
+        nc.scalar.activation(out=gain_sb[:, :, 2, :], in_=gain[:, :, HIGH, :], func=ACT.Copy, scale=-1.0)
+
+        w_columns = psum_acc.tile([P, 2, 2, HALF], F32, tag="acc")
+        for block in range(4):
+            nc.tensor.matmul(
+                out=w_columns[:, block // 2, block % 2, :],
+                lhsT=norm_w_rows[:, HALF * block : HALF * (block + 1)],
+                rhs=first_row[:],
+                start=True,
+                stop=True,
+            )
+        nc.vector.tensor_tensor(
+            out=scalers[:, TIMES_W : TIMES_W + 2].rearrange("p s t d -> p t s d"),
+            in0=w_columns[:],
+            in1=identity[:].unsqueeze(1).unsqueeze(1).to_broadcast([P, 2, 2, HALF]),
+            op=ALU.mult,
+        )
+        nc.vector.scalar_tensor_tensor(
+            out=scalers[:, MINUS_W_HIGH],
+            in0=w_columns[:, :, HIGH, :],
+            scalar=-1.0,
+            in1=identity[:].unsqueeze(1).to_broadcast([P, 2, HALF]),
+            op0=ALU.mult,
+            op1=ALU.mult,
+        )
+
+        def turn_angles(first, last):
+            turned_angles = psum_keep.tile([P, last - first, 4, P], BF16, tag="turned")
+            for m in range(first, last):
+                blocks = {
+                    ANGLE_PLACE[LOW][LOW]: cos_sb[:, m, 0:HALF],
+                    ANGLE_PLACE[LOW][HIGH]: sin_sb[:, m, 0:HALF],
+                    ANGLE_PLACE[HIGH][LOW]: sin_sb[:, m, HALF:D],
+                    ANGLE_PLACE[HIGH][HIGH]: cos_sb[:, m, HALF:D],
+                }
+                for place in range(4):
+                    nc.tensor.transpose(turned_angles[:, m - first, place, :], blocks[place], identity_bf[:])
+            angles_by_d = stage.tile([P, last - first, 4, P], BF16, tag="angles_by_d")
+            nc.scalar.copy(out=angles_by_d[:], in_=turned_angles[:])
+            return angles_by_d
+
+        def multiply_tables(m, angles, target):
+            made = psum_keep.tile([P, 2, 2, HALF], F32, tag="spare")
+            for source in (LOW, HIGH):
+                minus = target == LOW and source == HIGH
+                for step, place in enumerate(
+                    (MINUS_ONE if minus else PLUS_ONE, MINUS_W_HIGH if minus else TIMES_W + source)
+                ):
+                    nc.tensor.matmul(
+                        out=made[:, source].rearrange("p t d -> p (t d)"),
+                        lhsT=angles[:, ANGLE_PLACE[target][source], :],
+                        rhs=scalers[:, place].rearrange("p t d -> p (t d)"),
+                        start=(step == 0),
+                        stop=(step == 1),
+                    )
+            nc.scalar.copy(out=tables[:, m, :, target, :, :], in_=made[:].rearrange("p s t d -> p t s d"))
 
         def quantise_rows(first, last):
             grouped = stage.tile([P, last - first, PASSES * P * 4], BF16, align_bytes=64, tag="grouped")
@@ -164,22 +239,43 @@ def tile_gemmaattention_pa_kernel(
                 in_=grouped[:].rearrange("p m c -> p (m c)"),
             )
 
-        def build_tables(engine, gain_values, first, last):
+        def build_tables(on_vector, first, last):
             count = last - first
             angle = {
                 (LOW, LOW): cos_sb[:, first:last, 0:HALF],
-                (LOW, HIGH): minus_sin_low[:, first:last, :],
+                (LOW, HIGH): sin_sb[:, first:last, 0:HALF],
                 (HIGH, LOW): sin_sb[:, first:last, HALF:D],
                 (HIGH, HIGH): cos_sb[:, first:last, HALF:D],
             }
             for target in (LOW, HIGH):
                 for source in (LOW, HIGH):
-                    engine.tensor_tensor(
-                        out=tables[:, first:last, :, target, source, :],
-                        in0=gain_values[:, :, source, :].unsqueeze(1).to_broadcast([P, count, 2, HALF]),
-                        in1=angle[(target, source)].unsqueeze(2).to_broadcast([P, count, 2, HALF]),
-                        op=ALU.mult,
-                    )
+                    minus = target == LOW and source == HIGH
+                    some_tables = tables[:, first:last, :, target, source, :]
+                    some_angles = angle[(target, source)].unsqueeze(2).to_broadcast([P, count, 2, HALF])
+                    if on_vector and minus:
+                        for m in range(first, last):
+                            nc.vector.scalar_tensor_tensor(
+                                out=tables[:, m, :, target, source, :],
+                                in0=gain[:, :, source, :],
+                                scalar=-1.0,
+                                in1=sin_sb[:, m, 0:HALF].unsqueeze(1).to_broadcast([P, 2, HALF]),
+                                op0=ALU.mult,
+                                op1=ALU.mult,
+                            )
+                    elif on_vector:
+                        nc.vector.tensor_tensor(
+                            out=some_tables,
+                            in0=gain[:, :, source, :].unsqueeze(1).to_broadcast([P, count, 2, HALF]),
+                            in1=some_angles,
+                            op=ALU.mult,
+                        )
+                    else:
+                        nc.gpsimd.tensor_tensor(
+                            out=some_tables,
+                            in0=gain_sb[:, :, 2 if minus else source, :].unsqueeze(1).to_broadcast([P, count, 2, HALF]),
+                            in1=some_angles,
+                            op=ALU.mult,
+                        )
 
         def multiply(m, bank):
             acc = psum_acc.tile([P, BANK], F32)
@@ -237,18 +333,32 @@ def tile_gemmaattention_pa_kernel(
 
         def prepare(chunk):
             quantise_rows(chunk[0], chunk[1])
-            if chunk[0] < GPSIMD_TABLES_FROM:
-                build_tables(nc.vector, gain, chunk[0], min(chunk[1], GPSIMD_TABLES_FROM))
+            if chunk[0] < VECTOR_TABLES_TO:
+                build_tables(True, chunk[0], min(chunk[1], VECTOR_TABLES_TO))
 
         prepare(CHUNKS[0])
-        build_tables(nc.gpsimd, gain_sb, GPSIMD_TABLES_FROM, ROW_TILES)
+        build_tables(False, VECTOR_TABLES_TO, GPSIMD_TABLES_TO)
+        turned_for = {}
         for c in range(len(CHUNKS)):
             if c + 1 < len(CHUNKS):
                 prepare(CHUNKS[c + 1])
             for m in range(CHUNKS[c][0], CHUNKS[c][1]):
-                late_adder = nc.vector if m == ROW_TILES - 1 else nc.gpsimd
-                last_pieces = BANKS_PER_GROUP if m == ROW_TILES - 1 else 1
+                last = m == ROW_TILES - 1
+                q_high_adder = nc.vector if last and VECTOR_LAST_ADDS >= 2 else nc.gpsimd
+                k_adder = nc.vector if last and VECTOR_LAST_ADDS >= 1 else nc.gpsimd
+                last_pieces = BANKS_PER_GROUP if last else 1
+                ahead = m + TABLE_LEAD + 1
+                if GPSIMD_TABLES_TO <= ahead < ROW_TILES and (ahead - GPSIMD_TABLES_TO) % 2 == 0:
+                    both = turn_angles(ahead, ahead + 2)
+                    turned_for[ahead] = both[:, 0]
+                    turned_for[ahead + 1] = both[:, 1]
+                making = m + TABLE_LEAD
+                make_tables = GPSIMD_TABLES_TO <= making < ROW_TILES
                 norm_and_rope(m, Q_LOW_GROUP, Q_TABLE, nc.gpsimd, 1, q_rows[:, m, 0:GROUP_HEADS, :])
-                norm_and_rope(m, Q_HIGH_GROUP, Q_TABLE, late_adder, 1, q_rows[:, m, GROUP_HEADS:Q_HEADS, :])
+                if make_tables:
+                    multiply_tables(making, turned_for[making], LOW)
+                norm_and_rope(m, Q_HIGH_GROUP, Q_TABLE, q_high_adder, 1, q_rows[:, m, GROUP_HEADS:Q_HEADS, :])
+                if make_tables:
+                    multiply_tables(making, turned_for[making], HIGH)
                 copy_values(m)
-                norm_and_rope(m, K_GROUP, K_TABLE, late_adder, last_pieces, k_rows[:, m, :, :])
+                norm_and_rope(m, K_GROUP, K_TABLE, k_adder, last_pieces, k_rows[:, m, :, :])

@@ -43,7 +43,7 @@ CHUNKS = ((0, 1), (1, 2), (2, 4), (4, 8))
 VECTOR_TABLES_TO = 2
 GPSIMD_TABLES_TO = 4
 TABLE_LEAD = 2
-VECTOR_LAST_ADDS = 1
+ADDERS = {6: {1: "TG"}, 7: {0: "TG", 1: "TG", 2: "VV"}}
 PLUS_ONE = 0
 MINUS_ONE = 1
 TIMES_W = 2
@@ -291,7 +291,8 @@ def tile_gemmaattention_pa_kernel(
                 )
             return acc
 
-        def norm_and_rope(m, group, which_table, adder, pieces, destination):
+        def norm_and_rope(m, group, which_table, adders, destination):
+            pieces = len(adders)
             products = work.tile([P, GROUP_HEADS, 2, 2, HALF], F32)
             rotated = results.tile([P, GROUP_HEADS, 2, HALF], F32)
             for b in range(BANKS_PER_GROUP):
@@ -317,9 +318,25 @@ def tile_gemmaattention_pa_kernel(
                     )
                 if (b + 1) % (BANKS_PER_GROUP // pieces) == 0:
                     some = slice(HEADS_PER_BANK * (b + 1) - GROUP_HEADS // pieces, HEADS_PER_BANK * (b + 1))
-                    adder.tensor_tensor(
-                        out=rotated[:, some], in0=products[:, some, :, LOW, :], in1=products[:, some, :, HIGH, :], op=ALU.add
-                    )
+                    adder = adders[(b * pieces) // BANKS_PER_GROUP]
+                    if adder is None:
+                        total = psum_keep.tile([P, HEADS_PER_BANK, 2, HALF], F32, tag="spare")
+                        for source in (LOW, HIGH):
+                            nc.tensor.matmul(
+                                out=total[:],
+                                lhsT=identity[:],
+                                rhs=products[:, some, :, source, :],
+                                start=(source == LOW),
+                                stop=(source == HIGH),
+                            )
+                        nc.scalar.copy(out=rotated[:, some], in_=total[:])
+                    else:
+                        adder.tensor_tensor(
+                            out=rotated[:, some],
+                            in0=products[:, some, :, LOW, :],
+                            in1=products[:, some, :, HIGH, :],
+                            op=ALU.add,
+                        )
                     nc.sync.dma_start(
                         out=destination[:, some, :], in_=rotated[:, some].rearrange("p h t d -> p h (t d)")
                     )
@@ -343,10 +360,11 @@ def tile_gemmaattention_pa_kernel(
             if c + 1 < len(CHUNKS):
                 prepare(CHUNKS[c + 1])
             for m in range(CHUNKS[c][0], CHUNKS[c][1]):
-                last = m == ROW_TILES - 1
-                q_high_adder = nc.vector if last and VECTOR_LAST_ADDS >= 2 else nc.gpsimd
-                k_adder = nc.vector if last and VECTOR_LAST_ADDS >= 1 else nc.gpsimd
-                last_pieces = BANKS_PER_GROUP if last else 1
+                adders = dict(ADDERS.get(m, {}))
+                who = {"G": nc.gpsimd, "V": nc.vector, "T": None}
+                q_low_adders = tuple(who[a] for a in adders.get(Q_LOW_GROUP, "G"))
+                q_high_adders = tuple(who[a] for a in adders.get(Q_HIGH_GROUP, "G"))
+                k_adders = tuple(who[a] for a in adders.get(K_GROUP, "G"))
                 ahead = m + TABLE_LEAD + 1
                 if GPSIMD_TABLES_TO <= ahead < ROW_TILES and (ahead - GPSIMD_TABLES_TO) % 2 == 0:
                     both = turn_angles(ahead, ahead + 2)
@@ -354,11 +372,11 @@ def tile_gemmaattention_pa_kernel(
                     turned_for[ahead + 1] = both[:, 1]
                 making = m + TABLE_LEAD
                 make_tables = GPSIMD_TABLES_TO <= making < ROW_TILES
-                norm_and_rope(m, Q_LOW_GROUP, Q_TABLE, nc.gpsimd, 1, q_rows[:, m, 0:GROUP_HEADS, :])
+                norm_and_rope(m, Q_LOW_GROUP, Q_TABLE, q_low_adders, q_rows[:, m, 0:GROUP_HEADS, :])
                 if make_tables:
                     multiply_tables(making, turned_for[making], LOW)
-                norm_and_rope(m, Q_HIGH_GROUP, Q_TABLE, q_high_adder, 1, q_rows[:, m, GROUP_HEADS:Q_HEADS, :])
+                norm_and_rope(m, Q_HIGH_GROUP, Q_TABLE, q_high_adders, q_rows[:, m, GROUP_HEADS:Q_HEADS, :])
                 if make_tables:
                     multiply_tables(making, turned_for[making], HIGH)
                 copy_values(m)
-                norm_and_rope(m, K_GROUP, K_TABLE, k_adder, last_pieces, k_rows[:, m, :, :])
+                norm_and_rope(m, K_GROUP, K_TABLE, k_adders, k_rows[:, m, :, :])

@@ -40,7 +40,7 @@ V_GROUP = 3
 Q_TABLE = 0
 K_TABLE = 1
 CHUNKS = ((0, 1), (1, 2), (2, 4), (4, 8))
-VECTOR_TABLES_TO = 2
+VECTOR_TABLES_TO = 1
 GPSIMD_TABLES_TO = 4
 TABLE_LEAD = 2
 ADDERS = {6: {1: "TG"}, 7: {0: "TG", 1: "TG", 2: "VV"}}

@@ -41,7 +41,7 @@ Q_TABLE = 0
 K_TABLE = 1
 CHUNKS = ((0, 1), (1, 2), (2, 4), (4, 8))
 VECTOR_TABLES_TO = 1
-GPSIMD_TABLES_TO = 4
+GPSIMD_TABLES_TO = 5
 TABLE_LEAD = 2
 ADDERS = {6: {1: "TG"}, 7: {0: "TG", 1: "TG", 2: "VV"}}
 PLUS_ONE = 0
@@ -354,7 +354,8 @@ def tile_gemmaattention_pa_kernel(
                 build_tables(True, chunk[0], min(chunk[1], VECTOR_TABLES_TO))
 
         prepare(CHUNKS[0])
-        build_tables(False, VECTOR_TABLES_TO, GPSIMD_TABLES_TO)
+        build_tables(False, VECTOR_TABLES_TO, 3)
+        build_tables(False, 3, GPSIMD_TABLES_TO)
         turned_for = {}
         for c in range(len(CHUNKS)):
             if c + 1 < len(CHUNKS):
@@ -367,9 +368,9 @@ def tile_gemmaattention_pa_kernel(
                 k_adders = tuple(who[a] for a in adders.get(K_GROUP, "G"))
                 ahead = m + TABLE_LEAD + 1
                 if GPSIMD_TABLES_TO <= ahead < ROW_TILES and (ahead - GPSIMD_TABLES_TO) % 2 == 0:
-                    both = turn_angles(ahead, ahead + 2)
-                    turned_for[ahead] = both[:, 0]
-                    turned_for[ahead + 1] = both[:, 1]
+                    both = turn_angles(ahead, min(ahead + 2, ROW_TILES))
+                    for i in range(min(2, ROW_TILES - ahead)):
+                        turned_for[ahead + i] = both[:, i]
                 making = m + TABLE_LEAD
                 make_tables = GPSIMD_TABLES_TO <= making < ROW_TILES
                 norm_and_rope(m, Q_LOW_GROUP, Q_TABLE, q_low_adders, q_rows[:, m, 0:GROUP_HEADS, :])

@@ -73,7 +73,7 @@ def tile_gemmaattention_pa_kernel(
         work = ctx.enter_context(tc.tile_pool(name="work", bufs=6))
         results = ctx.enter_context(tc.tile_pool(name="results", bufs=4))
         psum_keep = ctx.enter_context(tc.psum_pool(name="psum_keep", bufs=1))
-        psum_acc = ctx.enter_context(tc.psum_pool(name="psum_acc", bufs=6))
+        psum_acc = ctx.enter_context(tc.psum_pool(name="psum_acc", bufs=7))
 
         hidden_sb = keep.tile([P, ROW_TILES, HID], BF16)
         cos_sb = keep.tile([P, ROW_TILES, D], BF16)
@@ -156,7 +156,7 @@ def tile_gemmaattention_pa_kernel(
         load_sin(GPSIMD_TABLES_TO, ROW_TILES)
         load_rows(4, 8)
 
-        gain = psum_keep.tile([P, 2, 2, HALF], F32, tag="spare")
+        gain = psum_acc.tile([P, 2, 2, HALF], F32, tag="acc")
         nc.tensor.matmul(
             out=gain[:].rearrange("p t h d -> p (t h d)"), lhsT=ones[:], rhs=norm_w_rows[:], start=True, stop=True
         )
@@ -189,7 +189,7 @@ def tile_gemmaattention_pa_kernel(
         )
 
         def turn_angles(first, last):
-            turned_angles = psum_keep.tile([P, last - first, 4, P], BF16, tag="turned")
+            turned_angles = psum_keep.tile([P, last - first, 4, P], BF16, tag="side")
             for m in range(first, last):
                 blocks = {
                     ANGLE_PLACE[LOW][LOW]: cos_sb[:, m, 0:HALF],
@@ -204,7 +204,7 @@ def tile_gemmaattention_pa_kernel(
             return angles_by_d
 
         def multiply_tables(m, angles, target):
-            made = psum_keep.tile([P, 2, 2, HALF], F32, tag="spare")
+            made = psum_keep.tile([P, 2, 2, HALF], F32, tag="side")
             for source in (LOW, HIGH):
                 minus = target == LOW and source == HIGH
                 for step, place in enumerate(
@@ -223,7 +223,7 @@ def tile_gemmaattention_pa_kernel(
             grouped = stage.tile([P, last - first, PASSES * P * 4], BF16, align_bytes=64, tag="grouped")
             for m in range(first, last):
                 pairs = hidden_sb[:, m, :].bitcast(F32)
-                turned = psum_keep.tile([P, PASSES, 2, P], F32)
+                turned = psum_keep.tile([P, PASSES, 2, P], F32, tag="side")
                 for g in range(PASSES):
                     for u in range(2):
                         nc.tensor.transpose(
@@ -320,7 +320,7 @@ def tile_gemmaattention_pa_kernel(
                     some = slice(HEADS_PER_BANK * (b + 1) - GROUP_HEADS // pieces, HEADS_PER_BANK * (b + 1))
                     adder = adders[(b * pieces) // BANKS_PER_GROUP]
                     if adder is None:
-                        total = psum_keep.tile([P, HEADS_PER_BANK, 2, HALF], F32, tag="spare")
+                        total = psum_keep.tile([P, HEADS_PER_BANK, 2, HALF], F32, tag="side")
                         for source in (LOW, HIGH):
                             nc.tensor.matmul(
                                 out=total[:],

@@ -69,9 +69,9 @@ def tile_gemmaattention_pa_kernel(
     with ExitStack() as ctx:
         keep = ctx.enter_context(tc.tile_pool(name="keep", bufs=1))
         stage = ctx.enter_context(tc.tile_pool(name="stage", bufs=2))
-        small = ctx.enter_context(tc.tile_pool(name="small", bufs=6))
-        work = ctx.enter_context(tc.tile_pool(name="work", bufs=6))
-        results = ctx.enter_context(tc.tile_pool(name="results", bufs=4))
+        small = ctx.enter_context(tc.tile_pool(name="small", bufs=10))
+        work = ctx.enter_context(tc.tile_pool(name="work", bufs=8))
+        results = ctx.enter_context(tc.tile_pool(name="results", bufs=5))
         psum_keep = ctx.enter_context(tc.psum_pool(name="psum_keep", bufs=1))
         psum_acc = ctx.enter_context(tc.psum_pool(name="psum_acc", bufs=7))
 

@@ -39,6 +39,8 @@ K_GROUP = 2
 V_GROUP = 3
 Q_TABLE = 0
 K_TABLE = 1
+WORD_PIECES = ((0, 1024), (1024, 2048), (2048, 3072), (3072, 4096))
+SCALE_PIECES = ((0, 1024), (1024, 4096))
 CHUNKS = ((0, 1), (1, 2), (2, 4), (4, 8))
 VECTOR_TABLES_TO = 1
 GPSIMD_TABLES_TO = 5
@@ -78,8 +80,12 @@ def tile_gemmaattention_pa_kernel(
         hidden_sb = keep.tile([P, ROW_TILES, HID], BF16)
         cos_sb = keep.tile([P, ROW_TILES, D], BF16)
         sin_sb = keep.tile([P, ROW_TILES, D], BF16)
-        w_words = keep.tile([P, PASSES, 2 * N_ALL], U8, align_bytes=64)
-        w_scales = keep.tile([P, PASSES, N_ALL], U8, align_bytes=64)
+        w_words = {}
+        for first, last in WORD_PIECES:
+            w_words[first] = keep.tile([P, PASSES, 2 * (last - first)], U8, align_bytes=64, name="w_words_%d" % first)
+        w_scales = {}
+        for first, last in SCALE_PIECES:
+            w_scales[first] = keep.tile([P, PASSES, last - first], U8, align_bytes=64, name="w_scales_%d" % first)
         x_words = keep.tile([P, ROW_TILES, PASSES * P], U32, align_bytes=64)
         x_scales = keep.tile([P, ROW_TILES, PASSES * P], U8, align_bytes=64)
         tables = keep.tile([P, ROW_TILES, 2, 2, 2, HALF], F32)
@@ -99,11 +105,11 @@ def tile_gemmaattention_pa_kernel(
         nc.vector.memset(first_row[0:1, :], 1.0)
         nc.vector.memset(eps[:], EPS)
 
-        def zero_scales(first, last):
-            nc.vector.memset(w_scales[:, :, first:last].bitcast(I32), 0)
+        def zero_scales(piece):
+            nc.vector.memset(w_scales[SCALE_PIECES[piece][0]][:].bitcast(I32), 0)
 
-        zero_scales(0, GROUP)
-        zero_scales(GROUP, N_ALL)
+        zero_scales(0)
+        zero_scales(1)
         make_identity(nc, identity[:])
         make_identity(nc, identity_bf[:])
         for place, sign in ((PLUS_ONE, 1.0), (MINUS_ONE, -1.0)):
@@ -126,17 +132,18 @@ def tile_gemmaattention_pa_kernel(
         def load_sin(first, last):
             nc.sync.dma_start(out=sin_sb[:, first:last, :], in_=sin_rows[:, first:last, :])
 
-        def load_scales(first, last):
+        def load_scales(piece):
+            first, last = SCALE_PIECES[piece]
             for r in range(4):
                 nc.sync.dma_start(
-                    out=w_scales[r : P : 32, :, first:last].bitcast(I32),
+                    out=w_scales[first][r : P : 32, :, :].bitcast(I32),
                     in_=w_qkv_scales[:, r : 16 : 4, first:last].rearrange("g q n -> q g n").bitcast(I32),
                 )
 
-        def load_words(group):
-            some = slice(2 * GROUP * group, 2 * GROUP * (group + 1))
+        def load_words(piece):
+            first, last = WORD_PIECES[piece]
             nc.sync.dma_start(
-                out=w_words[:, :, some].bitcast(I32), in_=words_by_partition[:, :, some].bitcast(I32)
+                out=w_words[first][:].bitcast(I32), in_=words_by_partition[:, :, 2 * first : 2 * last].bitcast(I32)
             )
 
         nc.sync.dma_start(out=norm_w_rows[0:1, 0:D], in_=q_norm_w.unsqueeze(0))
@@ -144,11 +151,11 @@ def tile_gemmaattention_pa_kernel(
         load_rows(0, 1)
         load_cos(0, GPSIMD_TABLES_TO)
         load_sin(0, GPSIMD_TABLES_TO)
-        load_scales(0, GROUP)
+        load_scales(0)
         load_words(Q_LOW_GROUP)
         load_words(Q_HIGH_GROUP)
         load_rows(1, 2)
-        load_scales(GROUP, N_ALL)
+        load_scales(1)
         load_words(V_GROUP)
         load_words(K_GROUP)
         load_rows(2, 4)
@@ -279,13 +286,18 @@ def tile_gemmaattention_pa_kernel(
 
         def multiply(m, bank):
             acc = psum_acc.tile([P, BANK], F32)
+            column = BANK * bank
+            words_at = max(first for first, last in WORD_PIECES if first <= column)
+            scales_at = max(first for first, last in SCALE_PIECES if first <= column)
+            some_words = slice(2 * (column - words_at), 2 * (column - words_at + BANK))
+            some_scales = slice(column - scales_at, column - scales_at + BANK)
             for g in range(PASSES):
                 nc.tensor.matmul_mx(
                     out=acc[:],
                     lhsT=x_words[:, m, P * g : P * (g + 1)].bitcast(FP8X4),
                     lhsT_scale=x_scales[:, m, P * g : P * (g + 1)],
-                    rhs=w_words[:, g, 2 * BANK * bank : 2 * BANK * (bank + 1)].bitcast(FP4X4),
-                    rhs_scale=w_scales[:, g, BANK * bank : BANK * (bank + 1)],
+                    rhs=w_words[words_at][:, g, some_words].bitcast(FP4X4),
+                    rhs_scale=w_scales[scales_at][:, g, some_scales],
                     start=(g == 0),
                     stop=(g == PASSES - 1),
                 )

@@ -42,7 +42,7 @@ K_TABLE = 1
 WORD_PIECES = ((0, 1024), (1024, 2048), (2048, 3072), (3072, 4096))
 SCALE_PIECES = ((0, 1024), (1024, 4096))
 CHUNKS = ((0, 1), (1, 2), (2, 4), (4, 8))
-VECTOR_TABLES_TO = 1
+VECTOR_TABLES_TO = 3
 GPSIMD_TABLES_TO = 5
 TABLE_LEAD = 2
 ADDERS = {6: {1: "TG"}, 7: {0: "TG", 1: "TG", 2: "VV"}}
@@ -360,18 +360,16 @@ def tile_gemmaattention_pa_kernel(
                 nc.scalar.copy(out=values[:, BANK * b : BANK * (b + 1)], in_=acc[:])
             nc.sync.dma_start(out=v_rows[:, m, :], in_=values[:])
 
-        def prepare(chunk):
-            quantise_rows(chunk[0], chunk[1])
-            if chunk[0] < VECTOR_TABLES_TO:
-                build_tables(True, chunk[0], min(chunk[1], VECTOR_TABLES_TO))
-
-        prepare(CHUNKS[0])
-        build_tables(False, VECTOR_TABLES_TO, 3)
-        build_tables(False, 3, GPSIMD_TABLES_TO)
+        with tc.manual_schedule(engines={mybir.EngineType.DVE}):
+            quantise_rows(*CHUNKS[0])
+            for m in range(VECTOR_TABLES_TO):
+                build_tables(True, m, m + 1)
+        for m in range(VECTOR_TABLES_TO, GPSIMD_TABLES_TO):
+            build_tables(False, m, m + 1)
         turned_for = {}
         for c in range(len(CHUNKS)):
-            if c + 1 < len(CHUNKS):
-                prepare(CHUNKS[c + 1])
+            if 0 < c < len(CHUNKS) - 1:
+                quantise_rows(*CHUNKS[c + 1])
             for m in range(CHUNKS[c][0], CHUNKS[c][1]):
                 adders = dict(ADDERS.get(m, {}))
                 who = {"G": nc.gpsimd, "V": nc.vector, "T": None}
@@ -386,6 +384,8 @@ def tile_gemmaattention_pa_kernel(
                 making = m + TABLE_LEAD
                 make_tables = GPSIMD_TABLES_TO <= making < ROW_TILES
                 norm_and_rope(m, Q_LOW_GROUP, Q_TABLE, q_low_adders, q_rows[:, m, 0:GROUP_HEADS, :])
+                if m == 0:
+                    quantise_rows(*CHUNKS[1])
                 if make_tables:
                     multiply_tables(making, turned_for[making], LOW)
                 norm_and_rope(m, Q_HIGH_GROUP, Q_TABLE, q_high_adders, q_rows[:, m, GROUP_HEADS:Q_HEADS, :])

@@ -151,14 +151,13 @@ def tile_gemmaattention_pa_kernel(
         load_rows(0, 1)
         load_cos(0, GPSIMD_TABLES_TO)
         load_sin(0, GPSIMD_TABLES_TO)
+        load_rows(1, 4)
         load_scales(0)
         load_words(Q_LOW_GROUP)
         load_words(Q_HIGH_GROUP)
-        load_rows(1, 2)
         load_scales(1)
         load_words(V_GROUP)
         load_words(K_GROUP)
-        load_rows(2, 4)
         load_cos(GPSIMD_TABLES_TO, ROW_TILES)
         load_sin(GPSIMD_TABLES_TO, ROW_TILES)
         load_rows(4, 8)
@@ -230,7 +229,10 @@ def tile_gemmaattention_pa_kernel(
             grouped = stage.tile([P, last - first, PASSES * P * 4], BF16, align_bytes=64, tag="grouped")
             for m in range(first, last):
                 pairs = hidden_sb[:, m, :].bitcast(F32)
-                turned = psum_keep.tile([P, PASSES, 2, P], F32, tag="side")
+                if m < CHUNKS[-1][0] and m % 2 == 1:
+                    turned = psum_acc.tile([P, PASSES, 2, P], F32, tag="acc")
+                else:
+                    turned = psum_keep.tile([P, PASSES, 2, P], F32, tag="side")
                 for g in range(PASSES):
                     for u in range(2):
                         nc.tensor.transpose(
@@ -361,15 +363,15 @@ def tile_gemmaattention_pa_kernel(
             nc.sync.dma_start(out=v_rows[:, m, :], in_=values[:])
 
         with tc.manual_schedule(engines={mybir.EngineType.DVE}):
-            quantise_rows(*CHUNKS[0])
             for m in range(VECTOR_TABLES_TO):
+                quantise_rows(*CHUNKS[m])
                 build_tables(True, m, m + 1)
         for m in range(VECTOR_TABLES_TO, GPSIMD_TABLES_TO):
             build_tables(False, m, m + 1)
         turned_for = {}
         for c in range(len(CHUNKS)):
-            if 0 < c < len(CHUNKS) - 1:
-                quantise_rows(*CHUNKS[c + 1])
+            if c + 1 == len(CHUNKS) - 1:
+                quantise_rows(*CHUNKS[-1])
             for m in range(CHUNKS[c][0], CHUNKS[c][1]):
                 adders = dict(ADDERS.get(m, {}))
                 who = {"G": nc.gpsimd, "V": nc.vector, "T": None}
@@ -384,8 +386,6 @@ def tile_gemmaattention_pa_kernel(
                 making = m + TABLE_LEAD
                 make_tables = GPSIMD_TABLES_TO <= making < ROW_TILES
                 norm_and_rope(m, Q_LOW_GROUP, Q_TABLE, q_low_adders, q_rows[:, m, 0:GROUP_HEADS, :])
-                if m == 0:
-                    quantise_rows(*CHUNKS[1])
                 if make_tables:
                     multiply_tables(making, turned_for[making], LOW)
                 norm_and_rope(m, Q_HIGH_GROUP, Q_TABLE, q_high_adders, q_rows[:, m, GROUP_HEADS:Q_HEADS, :])

@@ -42,10 +42,10 @@ K_TABLE = 1
 WORD_PIECES = ((0, 1024), (1024, 2048), (2048, 3072), (3072, 4096))
 SCALE_PIECES = ((0, 1024), (1024, 4096))
 CHUNKS = ((0, 1), (1, 2), (2, 4), (4, 8))
-VECTOR_TABLES_TO = 3
-GPSIMD_TABLES_TO = 5
+VECTOR_TABLES_TO = 2
+GPSIMD_TABLES_TO = 4
 TABLE_LEAD = 2
-ADDERS = {6: {1: "TG"}, 7: {0: "TG", 1: "TG", 2: "VV"}}
+ADDERS = {6: {1: "TG"}, 7: {0: "TG", 1: "TG", 2: "GV"}}
 PLUS_ONE = 0
 MINUS_ONE = 1
 TIMES_W = 2
@@ -98,10 +98,10 @@ def tile_gemmaattention_pa_kernel(
         eps = keep.tile([P, 1], F32)
         warm = keep.tile([P, 1], F32)
 
-        nc.vector.memset(norm_w_rows[:], 0.0)
+        nc.gpsimd.memset(norm_w_rows[:].bitcast(I32), 0)
         nc.vector.memset(norm_w_rows[32:33, :], 1.0)
         nc.vector.memset(ones[:], 1.0)
-        nc.vector.memset(first_row[:], 0.0)
+        nc.vector.memset(first_row[:].bitcast(I32), 0)
         nc.vector.memset(first_row[0:1, :], 1.0)
         nc.vector.memset(eps[:], EPS)
 
@@ -151,7 +151,8 @@ def tile_gemmaattention_pa_kernel(
         load_rows(0, 1)
         load_cos(0, GPSIMD_TABLES_TO)
         load_sin(0, GPSIMD_TABLES_TO)
-        load_rows(1, 4)
+        load_rows(1, 2)
+        load_rows(2, 4)
         load_scales(0)
         load_words(Q_LOW_GROUP)
         load_words(Q_HIGH_GROUP)
@@ -162,14 +163,6 @@ def tile_gemmaattention_pa_kernel(
         load_sin(GPSIMD_TABLES_TO, ROW_TILES)
         load_rows(4, 8)
 
-        gain = psum_acc.tile([P, 2, 2, HALF], F32, tag="acc")
-        nc.tensor.matmul(
-            out=gain[:].rearrange("p t h d -> p (t h d)"), lhsT=ones[:], rhs=norm_w_rows[:], start=True, stop=True
-        )
-        gain_sb = keep.tile([P, 2, 3, HALF], F32)
-        nc.scalar.copy(out=gain_sb[:, :, 0:2, :], in_=gain[:])
-        nc.scalar.activation(out=gain_sb[:, :, 2, :], in_=gain[:, :, HIGH, :], func=ACT.Copy, scale=-1.0)
-
         w_columns = psum_acc.tile([P, 2, 2, HALF], F32, tag="acc")
         for block in range(4):
             nc.tensor.matmul(
@@ -179,20 +172,22 @@ def tile_gemmaattention_pa_kernel(
                 start=True,
                 stop=True,
             )
-        nc.vector.tensor_tensor(
-            out=scalers[:, TIMES_W : TIMES_W + 2].rearrange("p s t d -> p t s d"),
-            in0=w_columns[:],
-            in1=identity[:].unsqueeze(1).unsqueeze(1).to_broadcast([P, 2, 2, HALF]),
-            op=ALU.mult,
+
+        gain = psum_acc.tile([P, 2, 2, HALF], F32, tag="acc")
+        nc.tensor.matmul(
+            out=gain[:].rearrange("p t h d -> p (t h d)"), lhsT=ones[:], rhs=norm_w_rows[:], start=True, stop=True
         )
-        nc.vector.scalar_tensor_tensor(
-            out=scalers[:, MINUS_W_HIGH],
-            in0=w_columns[:, :, HIGH, :],
-            scalar=-1.0,
-            in1=identity[:].unsqueeze(1).to_broadcast([P, 2, HALF]),
-            op0=ALU.mult,
-            op1=ALU.mult,
+        gain_again = psum_acc.tile([P, 2, 2, HALF], F32, tag="acc")
+        nc.tensor.matmul(
+            out=gain_again[:].rearrange("p t h d -> p (t h d)"),
+            lhsT=ones[:],
+            rhs=norm_w_rows[:],
+            start=True,
+            stop=True,
         )
+        gain_sb = keep.tile([P, 2, 3, HALF], F32)
+        nc.scalar.copy(out=gain_sb[:, :, 0:2, :], in_=gain_again[:])
+        nc.scalar.activation(out=gain_sb[:, :, 2, :], in_=gain_again[:, :, HIGH, :], func=ACT.Copy, scale=-1.0)
 
         def turn_angles(first, last):
             turned_angles = psum_keep.tile([P, last - first, 4, P], BF16, tag="side")
@@ -363,9 +358,25 @@ def tile_gemmaattention_pa_kernel(
             nc.sync.dma_start(out=v_rows[:, m, :], in_=values[:])
 
         with tc.manual_schedule(engines={mybir.EngineType.DVE}):
-            for m in range(VECTOR_TABLES_TO):
-                quantise_rows(*CHUNKS[m])
-                build_tables(True, m, m + 1)
+            nc.vector.tensor_tensor(
+                out=scalers[:, TIMES_W : TIMES_W + 2].rearrange("p s t d -> p t s d"),
+                in0=w_columns[:],
+                in1=identity[:].unsqueeze(1).unsqueeze(1).to_broadcast([P, 2, 2, HALF]),
+                op=ALU.mult,
+            )
+            nc.vector.scalar_tensor_tensor(
+                out=scalers[:, MINUS_W_HIGH],
+                in0=w_columns[:, :, HIGH, :],
+                scalar=-1.0,
+                in1=identity[:].unsqueeze(1).to_broadcast([P, 2, HALF]),
+                op0=ALU.mult,
+                op1=ALU.mult,
+            )
+            build_tables(True, 0, 1)
+            quantise_rows(*CHUNKS[0])
+            build_tables(True, 1, VECTOR_TABLES_TO)
+            quantise_rows(*CHUNKS[1])
+            quantise_rows(*CHUNKS[2])
         for m in range(VECTOR_TABLES_TO, GPSIMD_TABLES_TO):
             build_tables(False, m, m + 1)
         turned_for = {}

@@ -42,8 +42,8 @@ K_TABLE = 1
 WORD_PIECES = ((0, 1024), (1024, 2048), (2048, 3072), (3072, 4096))
 SCALE_PIECES = ((0, 1024), (1024, 4096))
 CHUNKS = ((0, 1), (1, 2), (2, 4), (4, 8))
-VECTOR_TABLES_TO = 2
-GPSIMD_TABLES_TO = 4
+VECTOR_TABLES_TO = 3
+GPSIMD_TABLES_TO = 5
 TABLE_LEAD = 2
 ADDERS = {6: {1: "TG"}, 7: {0: "TG", 1: "TG", 2: "GV"}}
 PLUS_ONE = 0
@@ -300,19 +300,21 @@ def tile_gemmaattention_pa_kernel(
                 )
             return acc
 
+        unfinished = []
+
+        def finish_last():
+            ready = list(unfinished)
+            unfinished.clear()
+            for finish in ready:
+                finish()
+
         def norm_and_rope(m, group, which_table, adders, destination):
             pieces = len(adders)
             products = work.tile([P, GROUP_HEADS, 2, 2, HALF], F32)
             rotated = results.tile([P, GROUP_HEADS, 2, HALF], F32)
-            for b in range(BANKS_PER_GROUP):
-                acc = multiply(m, BANKS_PER_GROUP * group + b)
-                sum_sq = small.tile([P, HEADS_PER_BANK], F32)
+
+            def finish(b, acc, sum_sq):
                 rstd = small.tile([P, HEADS_PER_BANK], F32)
-                for h in range(HEADS_PER_BANK):
-                    squares = stage.tile([P, D], BF16, bufs=4)
-                    nc.scalar.activation(
-                        out=squares[:], in_=acc[:, D * h : D * (h + 1)], func=ACT.Square, accum_out=sum_sq[:, h : h + 1]
-                    )
                 nc.scalar.activation(
                     out=rstd[:], in_=sum_sq[:], func=ACT.Abs_reciprocal_sqrt, scale=1.0 / D, bias=eps[:]
                 )
@@ -325,36 +327,51 @@ def tile_gemmaattention_pa_kernel(
                         op0=ALU.mult,
                         op1=ALU.mult,
                     )
-                if (b + 1) % (BANKS_PER_GROUP // pieces) == 0:
-                    some = slice(HEADS_PER_BANK * (b + 1) - GROUP_HEADS // pieces, HEADS_PER_BANK * (b + 1))
-                    adder = adders[(b * pieces) // BANKS_PER_GROUP]
-                    if adder is None:
-                        total = psum_keep.tile([P, HEADS_PER_BANK, 2, HALF], F32, tag="side")
-                        for source in (LOW, HIGH):
-                            nc.tensor.matmul(
-                                out=total[:],
-                                lhsT=identity[:],
-                                rhs=products[:, some, :, source, :],
-                                start=(source == LOW),
-                                stop=(source == HIGH),
-                            )
-                        nc.scalar.copy(out=rotated[:, some], in_=total[:])
-                    else:
-                        adder.tensor_tensor(
-                            out=rotated[:, some],
-                            in0=products[:, some, :, LOW, :],
-                            in1=products[:, some, :, HIGH, :],
-                            op=ALU.add,
+                if (b + 1) % (BANKS_PER_GROUP // pieces) != 0:
+                    return
+                some = slice(HEADS_PER_BANK * (b + 1) - GROUP_HEADS // pieces, HEADS_PER_BANK * (b + 1))
+                adder = adders[(b * pieces) // BANKS_PER_GROUP]
+                if adder is None:
+                    total = psum_keep.tile([P, HEADS_PER_BANK, 2, HALF], F32, tag="side")
+                    for source in (LOW, HIGH):
+                        nc.tensor.matmul(
+                            out=total[:],
+                            lhsT=identity[:],
+                            rhs=products[:, some, :, source, :],
+                            start=(source == LOW),
+                            stop=(source == HIGH),
                         )
-                    nc.sync.dma_start(
-                        out=destination[:, some, :], in_=rotated[:, some].rearrange("p h t d -> p h (t d)")
+                    nc.scalar.copy(out=rotated[:, some], in_=total[:])
+                else:
+                    adder.tensor_tensor(
+                        out=rotated[:, some],
+                        in0=products[:, some, :, LOW, :],
+                        in1=products[:, some, :, HIGH, :],
+                        op=ALU.add,
                     )
+                nc.sync.dma_start(
+                    out=destination[:, some, :], in_=rotated[:, some].rearrange("p h t d -> p h (t d)")
+                )
+
+            for b in range(BANKS_PER_GROUP):
+                acc = multiply(m, BANKS_PER_GROUP * group + b)
+                sum_sq = small.tile([P, HEADS_PER_BANK], F32)
+                for h in range(HEADS_PER_BANK):
+                    squares = stage.tile([P, D], BF16, bufs=4)
+                    nc.scalar.activation(
+                        out=squares[:], in_=acc[:, D * h : D * (h + 1)], func=ACT.Square, accum_out=sum_sq[:, h : h + 1]
+                    )
+                    finish_last()
+                unfinished.append(lambda b=b, acc=acc, sum_sq=sum_sq: finish(b, acc, sum_sq))
+                if m == 0 and group == Q_LOW_GROUP:
+                    finish_last()
 
         def copy_values(m):
             values = results.tile([P, GROUP], F32)
             for b in range(BANKS_PER_GROUP):
                 acc = multiply(m, BANKS_PER_GROUP * V_GROUP + b)
                 nc.scalar.copy(out=values[:, BANK * b : BANK * (b + 1)], in_=acc[:])
+                finish_last()
             nc.sync.dma_start(out=v_rows[:, m, :], in_=values[:])
 
         with tc.manual_schedule(engines={mybir.EngineType.DVE}):
@@ -374,9 +391,10 @@ def tile_gemmaattention_pa_kernel(
             )
             build_tables(True, 0, 1)
             quantise_rows(*CHUNKS[0])
-            build_tables(True, 1, VECTOR_TABLES_TO)
+            build_tables(True, 1, 2)
             quantise_rows(*CHUNKS[1])
             quantise_rows(*CHUNKS[2])
+            build_tables(True, 2, VECTOR_TABLES_TO)
         for m in range(VECTOR_TABLES_TO, GPSIMD_TABLES_TO):
             build_tables(False, m, m + 1)
         turned_for = {}
@@ -404,3 +422,4 @@ def tile_gemmaattention_pa_kernel(
                     multiply_tables(making, turned_for[making], HIGH)
                 copy_values(m)
                 norm_and_rope(m, K_GROUP, K_TABLE, k_adders, k_rows[:, m, :, :])
+        finish_last()

from contextlib import ExitStack

import concourse.mybir as mybir
from concourse.masks import make_identity

F32 = mybir.dt.float32
BF16 = mybir.dt.bfloat16
I32 = mybir.dt.int32
U32 = mybir.dt.uint32
U8 = mybir.dt.uint8
FP8X4 = mybir.dt.float8_e4m3fn_x4
FP4X4 = mybir.dt.float4_e2m1fn_x4
ACT = mybir.ActivationFunctionType
ALU = mybir.AluOpType

P = 128
S = 1024
HID = 1024
D = 256
HALF = D // 2
LOW = 0
HIGH = 1
Q_HEADS = 8
KV_HEADS = 4
N_ALL = (Q_HEADS + 2 * KV_HEADS) * D
EPS = 1e-6

K_PASS = 512
PASSES = HID // K_PASS
ROW_TILES = S // P
BANK = 512
HEADS_PER_BANK = BANK // D
GROUP_HEADS = 4
GROUP = GROUP_HEADS * D
BANKS_PER_GROUP = GROUP // BANK
Q_LOW_GROUP = 0
Q_HIGH_GROUP = 1
K_GROUP = 2
V_GROUP = 3
Q_TABLE = 0
K_TABLE = 1
WORD_PIECES = ((0, 1024), (1024, 2048), (2048, 3072), (3072, 4096))
SCALE_PIECES = ((0, 1024), (1024, 4096))
CHUNKS = ((0, 1), (1, 2), (2, 4), (4, 8))
VECTOR_TABLES_TO = 3
GPSIMD_TABLES_TO = 5
TABLE_LEAD = 2
ADDERS = {6: {1: "TG"}, 7: {0: "TG", 1: "TG", 2: "GV"}}
PLUS_ONE = 0
MINUS_ONE = 1
TIMES_W = 2
MINUS_W_HIGH = 4
ANGLE_PLACE = ((0, 1), (2, 3))

FLOPS = 2 * S * HID * N_ALL


def tile_gemmaattention_pa_kernel(
    tc, hidden_states, w_qkv_words, w_qkv_scales, q_norm_w, k_norm_w, cos, sin, out_0, out_1, out_2
):
    nc = tc.nc

    hidden_rows = hidden_states.rearrange("(p m) k -> p m k", m=ROW_TILES)
    cos_rows = cos.rearrange("(p m) d -> p m d", m=ROW_TILES)
    sin_rows = sin.rearrange("(p m) d -> p m d", m=ROW_TILES)
    q_rows = out_0.rearrange("(p m) h d -> p m h d", m=ROW_TILES)
    k_rows = out_1.rearrange("(p m) h d -> p m h d", m=ROW_TILES)
    v_rows = out_2.rearrange("(p m) h d -> p m (h d)", m=ROW_TILES)
    words_by_partition = w_qkv_words.rearrange("g p b -> p g b")

    with ExitStack() as ctx:
        keep = ctx.enter_context(tc.tile_pool(name="keep", bufs=1))
        stage = ctx.enter_context(tc.tile_pool(name="stage", bufs=2))
        small = ctx.enter_context(tc.tile_pool(name="small", bufs=10))
        work = ctx.enter_context(tc.tile_pool(name="work", bufs=8))
        results = ctx.enter_context(tc.tile_pool(name="results", bufs=5))
        psum_keep = ctx.enter_context(tc.psum_pool(name="psum_keep", bufs=1))
        psum_acc = ctx.enter_context(tc.psum_pool(name="psum_acc", bufs=7))

        hidden_sb = keep.tile([P, ROW_TILES, HID], BF16)
        cos_sb = keep.tile([P, ROW_TILES, D], BF16)
        sin_sb = keep.tile([P, ROW_TILES, D], BF16)
        w_words = {}
        for first, last in WORD_PIECES:
            w_words[first] = keep.tile([P, PASSES, 2 * (last - first)], U8, align_bytes=64, name="w_words_%d" % first)
        w_scales = {}
        for first, last in SCALE_PIECES:
            w_scales[first] = keep.tile([P, PASSES, last - first], U8, align_bytes=64, name="w_scales_%d" % first)
        x_words = keep.tile([P, ROW_TILES, PASSES * P], U32, align_bytes=64)
        x_scales = keep.tile([P, ROW_TILES, PASSES * P], U8, align_bytes=64)
        tables = keep.tile([P, ROW_TILES, 2, 2, 2, HALF], F32)
        identity = keep.tile([P, P], F32)
        identity_bf = keep.tile([P, P], BF16)
        first_row = keep.tile([P, P], BF16)
        scalers = keep.tile([P, 5, 2, HALF], BF16)
        ones = keep.tile([P, P], BF16)
        norm_w_rows = keep.tile([P, 2 * D], BF16)
        eps = keep.tile([P, 1], F32)
        warm = keep.tile([P, 1], F32)

        nc.gpsimd.memset(norm_w_rows[:].bitcast(I32), 0)
        nc.vector.memset(norm_w_rows[32:33, :], 1.0)
        nc.vector.memset(ones[:], 1.0)
        nc.vector.memset(first_row[:].bitcast(I32), 0)
        nc.vector.memset(first_row[0:1, :], 1.0)
        nc.vector.memset(eps[:], EPS)

        def zero_scales(piece):
            nc.vector.memset(w_scales[SCALE_PIECES[piece][0]][:].bitcast(I32), 0)

        zero_scales(0)
        zero_scales(1)
        make_identity(nc, identity[:])
        make_identity(nc, identity_bf[:])
        for place, sign in ((PLUS_ONE, 1.0), (MINUS_ONE, -1.0)):
            nc.gpsimd.tensor_scalar(
                out=scalers[:, place],
                in0=identity[:].unsqueeze(1).to_broadcast([P, 2, HALF]),
                scalar1=sign,
                scalar2=0.0,
                op0=ALU.mult,
                op1=ALU.add,
            )
        nc.scalar.activation(out=warm[:], in_=eps[:], func=ACT.Abs_reciprocal_sqrt)

        def load_rows(first, last):
            nc.sync.dma_start(out=hidden_sb[:, first:last, :], in_=hidden_rows[:, first:last, :])

        def load_cos(first, last):
            nc.sync.dma_start(out=cos_sb[:, first:last, :], in_=cos_rows[:, first:last, :])

        def load_sin(first, last):
            nc.sync.dma_start(out=sin_sb[:, first:last, :], in_=sin_rows[:, first:last, :])

        def load_scales(piece):
            first, last = SCALE_PIECES[piece]
            for r in range(4):
                nc.sync.dma_start(
                    out=w_scales[first][r : P : 32, :, :].bitcast(I32),
                    in_=w_qkv_scales[:, r : 16 : 4, first:last].rearrange("g q n -> q g n").bitcast(I32),
                )

        def load_words(piece):
            first, last = WORD_PIECES[piece]
            nc.sync.dma_start(
                out=w_words[first][:].bitcast(I32), in_=words_by_partition[:, :, 2 * first : 2 * last].bitcast(I32)
            )

        nc.sync.dma_start(out=norm_w_rows[0:1, 0:D], in_=q_norm_w.unsqueeze(0))
        nc.sync.dma_start(out=norm_w_rows[0:1, D : 2 * D], in_=k_norm_w.unsqueeze(0))
        load_rows(0, 1)
        load_cos(0, GPSIMD_TABLES_TO)
        load_sin(0, GPSIMD_TABLES_TO)
        load_rows(1, 2)
        load_rows(2, 4)
        load_scales(0)
        load_words(Q_LOW_GROUP)
        load_words(Q_HIGH_GROUP)
        load_scales(1)
        load_words(V_GROUP)
        load_words(K_GROUP)
        load_cos(GPSIMD_TABLES_TO, ROW_TILES)
        load_sin(GPSIMD_TABLES_TO, ROW_TILES)
        load_rows(4, 8)

        w_columns = psum_acc.tile([P, 2, 2, HALF], F32, tag="acc")
        for block in range(4):
            nc.tensor.matmul(
                out=w_columns[:, block // 2, block % 2, :],
                lhsT=norm_w_rows[:, HALF * block : HALF * (block + 1)],
                rhs=first_row[:],
                start=True,
                stop=True,
            )

        gain = psum_acc.tile([P, 2, 2, HALF], F32, tag="acc")
        nc.tensor.matmul(
            out=gain[:].rearrange("p t h d -> p (t h d)"), lhsT=ones[:], rhs=norm_w_rows[:], start=True, stop=True
        )
        gain_again = psum_acc.tile([P, 2, 2, HALF], F32, tag="acc")
        nc.tensor.matmul(
            out=gain_again[:].rearrange("p t h d -> p (t h d)"),
            lhsT=ones[:],
            rhs=norm_w_rows[:],
            start=True,
            stop=True,
        )
        gain_sb = keep.tile([P, 2, 3, HALF], F32)
        nc.scalar.copy(out=gain_sb[:, :, 0:2, :], in_=gain_again[:])
        nc.scalar.activation(out=gain_sb[:, :, 2, :], in_=gain_again[:, :, HIGH, :], func=ACT.Copy, scale=-1.0)

        def turn_angles(first, last):
            turned_angles = psum_keep.tile([P, last - first, 4, P], BF16, tag="side")
            for m in range(first, last):
                blocks = {
                    ANGLE_PLACE[LOW][LOW]: cos_sb[:, m, 0:HALF],
                    ANGLE_PLACE[LOW][HIGH]: sin_sb[:, m, 0:HALF],
                    ANGLE_PLACE[HIGH][LOW]: sin_sb[:, m, HALF:D],
                    ANGLE_PLACE[HIGH][HIGH]: cos_sb[:, m, HALF:D],
                }
                for place in range(4):
                    nc.tensor.transpose(turned_angles[:, m - first, place, :], blocks[place], identity_bf[:])
            angles_by_d = stage.tile([P, last - first, 4, P], BF16, tag="angles_by_d")
            nc.scalar.copy(out=angles_by_d[:], in_=turned_angles[:])
            return angles_by_d

        def multiply_tables(m, angles, target):
            made = psum_keep.tile([P, 2, 2, HALF], F32, tag="side")
            for source in (LOW, HIGH):
                minus = target == LOW and source == HIGH
                for step, place in enumerate(
                    (MINUS_ONE if minus else PLUS_ONE, MINUS_W_HIGH if minus else TIMES_W + source)
                ):
                    nc.tensor.matmul(
                        out=made[:, source].rearrange("p t d -> p (t d)"),
                        lhsT=angles[:, ANGLE_PLACE[target][source], :],
                        rhs=scalers[:, place].rearrange("p t d -> p (t d)"),
                        start=(step == 0),
                        stop=(step == 1),
                    )
            nc.scalar.copy(out=tables[:, m, :, target, :, :], in_=made[:].rearrange("p s t d -> p t s d"))

        def quantise_rows(first, last):
            grouped = stage.tile([P, last - first, PASSES * P * 4], BF16, align_bytes=64, tag="grouped")
            for m in range(first, last):
                pairs = hidden_sb[:, m, :].bitcast(F32)
                if m < CHUNKS[-1][0] and m % 2 == 1:
                    turned = psum_acc.tile([P, PASSES, 2, P], F32, tag="acc")
                else:
                    turned = psum_keep.tile([P, PASSES, 2, P], F32, tag="side")
                for g in range(PASSES):
                    for u in range(2):
                        nc.tensor.transpose(
                            turned[:, g, u, :], pairs[:, 256 * g + u : 256 * (g + 1) : 2], identity[:]
                        )
                nc.scalar.copy(
                    out=grouped[:, m - first, :].bitcast(F32).rearrange("p (g r u) -> p g r u", g=PASSES, u=2),
                    in_=turned[:].rearrange("p g u r -> p g r u"),
                )
            nc.vector.quantize_mx(
                out=x_words[:, first:last, :].rearrange("p m c -> p (m c)").bitcast(FP8X4),
                scales=x_scales[:, first:last, :].rearrange("p m c -> p (m c)"),
                in_=grouped[:].rearrange("p m c -> p (m c)"),
            )

        def build_tables(on_vector, first, last):
            count = last - first
            angle = {
                (LOW, LOW): cos_sb[:, first:last, 0:HALF],
                (LOW, HIGH): sin_sb[:, first:last, 0:HALF],
                (HIGH, LOW): sin_sb[:, first:last, HALF:D],
                (HIGH, HIGH): cos_sb[:, first:last, HALF:D],
            }
            for target in (LOW, HIGH):
                for source in (LOW, HIGH):
                    minus = target == LOW and source == HIGH
                    some_tables = tables[:, first:last, :, target, source, :]
                    some_angles = angle[(target, source)].unsqueeze(2).to_broadcast([P, count, 2, HALF])
                    if on_vector and minus:
                        for m in range(first, last):
                            nc.vector.scalar_tensor_tensor(
                                out=tables[:, m, :, target, source, :],
                                in0=gain[:, :, source, :],
                                scalar=-1.0,
                                in1=sin_sb[:, m, 0:HALF].unsqueeze(1).to_broadcast([P, 2, HALF]),
                                op0=ALU.mult,
                                op1=ALU.mult,
                            )
                    elif on_vector:
                        nc.vector.tensor_tensor(
                            out=some_tables,
                            in0=gain[:, :, source, :].unsqueeze(1).to_broadcast([P, count, 2, HALF]),
                            in1=some_angles,
                            op=ALU.mult,
                        )
                    else:
                        nc.gpsimd.tensor_tensor(
                            out=some_tables,
                            in0=gain_sb[:, :, 2 if minus else source, :].unsqueeze(1).to_broadcast([P, count, 2, HALF]),
                            in1=some_angles,
                            op=ALU.mult,
                        )

        def multiply(m, bank):
            acc = psum_acc.tile([P, BANK], F32)
            column = BANK * bank
            words_at = max(first for first, last in WORD_PIECES if first <= column)
            scales_at = max(first for first, last in SCALE_PIECES if first <= column)
            some_words = slice(2 * (column - words_at), 2 * (column - words_at + BANK))
            some_scales = slice(column - scales_at, column - scales_at + BANK)
            for g in range(PASSES):
                nc.tensor.matmul_mx(
                    out=acc[:],
                    lhsT=x_words[:, m, P * g : P * (g + 1)].bitcast(FP8X4),
                    lhsT_scale=x_scales[:, m, P * g : P * (g + 1)],
                    rhs=w_words[words_at][:, g, some_words].bitcast(FP4X4),
                    rhs_scale=w_scales[scales_at][:, g, some_scales],
                    start=(g == 0),
                    stop=(g == PASSES - 1),
                )
            return acc

        unfinished = []

        def finish_last():
            ready = list(unfinished)
            unfinished.clear()
            for finish in ready:
                finish()

        def norm_and_rope(m, group, which_table, adders, destination):
            pieces = len(adders)
            products = work.tile([P, GROUP_HEADS, 2, 2, HALF], F32)
            rotated = results.tile([P, GROUP_HEADS, 2, HALF], F32)

            def finish(b, acc, sum_sq):
                rstd = small.tile([P, HEADS_PER_BANK], F32)
                nc.scalar.activation(
                    out=rstd[:], in_=sum_sq[:], func=ACT.Abs_reciprocal_sqrt, scale=1.0 / D, bias=eps[:]
                )
                for h in range(HEADS_PER_BANK):
                    nc.vector.scalar_tensor_tensor(
                        out=products[:, HEADS_PER_BANK * b + h].rearrange("p t s d -> p t (s d)"),
                        in0=acc[:, D * h : D * (h + 1)].unsqueeze(1).to_broadcast([P, 2, D]),
                        scalar=rstd[:, h : h + 1],
                        in1=tables[:, m, which_table].rearrange("p t s d -> p t (s d)"),
                        op0=ALU.mult,
                        op1=ALU.mult,
                    )
                if (b + 1) % (BANKS_PER_GROUP // pieces) != 0:
                    return
                some = slice(HEADS_PER_BANK * (b + 1) - GROUP_HEADS // pieces, HEADS_PER_BANK * (b + 1))
                adder = adders[(b * pieces) // BANKS_PER_GROUP]
                if adder is None:
                    total = psum_keep.tile([P, HEADS_PER_BANK, 2, HALF], F32, tag="side")
                    for source in (LOW, HIGH):
                        nc.tensor.matmul(
                            out=total[:],
                            lhsT=identity[:],
                            rhs=products[:, some, :, source, :],
                            start=(source == LOW),
                            stop=(source == HIGH),
                        )
                    nc.scalar.copy(out=rotated[:, some], in_=total[:])
                else:
                    adder.tensor_tensor(
                        out=rotated[:, some],
                        in0=products[:, some, :, LOW, :],
                        in1=products[:, some, :, HIGH, :],
                        op=ALU.add,
                    )
                nc.sync.dma_start(
                    out=destination[:, some, :], in_=rotated[:, some].rearrange("p h t d -> p h (t d)")
                )

            for b in range(BANKS_PER_GROUP):
                acc = multiply(m, BANKS_PER_GROUP * group + b)
                sum_sq = small.tile([P, HEADS_PER_BANK], F32)
                for h in range(HEADS_PER_BANK):
                    squares = stage.tile([P, D], BF16, bufs=4)
                    nc.scalar.activation(
                        out=squares[:], in_=acc[:, D * h : D * (h + 1)], func=ACT.Square, accum_out=sum_sq[:, h : h + 1]
                    )
                    finish_last()
                unfinished.append(lambda b=b, acc=acc, sum_sq=sum_sq: finish(b, acc, sum_sq))
                if m == 0 and group == Q_LOW_GROUP:
                    finish_last()

        def copy_values(m):
            values = results.tile([P, GROUP], F32)
            for b in range(BANKS_PER_GROUP):
                acc = multiply(m, BANKS_PER_GROUP * V_GROUP + b)
                nc.scalar.copy(out=values[:, BANK * b : BANK * (b + 1)], in_=acc[:])
                finish_last()
            nc.sync.dma_start(out=v_rows[:, m, :], in_=values[:])

        with tc.manual_schedule(engines={mybir.EngineType.DVE}):
            nc.vector.tensor_tensor(
                out=scalers[:, TIMES_W : TIMES_W + 2].rearrange("p s t d -> p t s d"),
                in0=w_columns[:],
                in1=identity[:].unsqueeze(1).unsqueeze(1).to_broadcast([P, 2, 2, HALF]),
                op=ALU.mult,
            )
            nc.vector.scalar_tensor_tensor(
                out=scalers[:, MINUS_W_HIGH],
                in0=w_columns[:, :, HIGH, :],
                scalar=-1.0,
                in1=identity[:].unsqueeze(1).to_broadcast([P, 2, HALF]),
                op0=ALU.mult,
                op1=ALU.mult,
            )
            build_tables(True, 0, 1)
            quantise_rows(*CHUNKS[0])
            build_tables(True, 1, 2)
            quantise_rows(*CHUNKS[1])
            quantise_rows(*CHUNKS[2])
            build_tables(True, 2, VECTOR_TABLES_TO)
        for m in range(VECTOR_TABLES_TO, GPSIMD_TABLES_TO):
            build_tables(False, m, m + 1)
        turned_for = {}
        for c in range(len(CHUNKS)):
            if c + 1 == len(CHUNKS) - 1:
                quantise_rows(*CHUNKS[-1])
            for m in range(CHUNKS[c][0], CHUNKS[c][1]):
                adders = dict(ADDERS.get(m, {}))
                who = {"G": nc.gpsimd, "V": nc.vector, "T": None}
                q_low_adders = tuple(who[a] for a in adders.get(Q_LOW_GROUP, "G"))
                q_high_adders = tuple(who[a] for a in adders.get(Q_HIGH_GROUP, "G"))
                k_adders = tuple(who[a] for a in adders.get(K_GROUP, "G"))
                ahead = m + TABLE_LEAD + 1
                if GPSIMD_TABLES_TO <= ahead < ROW_TILES and (ahead - GPSIMD_TABLES_TO) % 2 == 0:
                    both = turn_angles(ahead, min(ahead + 2, ROW_TILES))
                    for i in range(min(2, ROW_TILES - ahead)):
                        turned_for[ahead + i] = both[:, i]
                making = m + TABLE_LEAD
                make_tables = GPSIMD_TABLES_TO <= making < ROW_TILES
                norm_and_rope(m, Q_LOW_GROUP, Q_TABLE, q_low_adders, q_rows[:, m, 0:GROUP_HEADS, :])
                if make_tables:
                    multiply_tables(making, turned_for[making], LOW)
                norm_and_rope(m, Q_HIGH_GROUP, Q_TABLE, q_high_adders, q_rows[:, m, GROUP_HEADS:Q_HEADS, :])
                if make_tables:
                    multiply_tables(making, turned_for[making], HIGH)
                copy_values(m)
                norm_and_rope(m, K_GROUP, K_TABLE, k_adders, k_rows[:, m, :, :])
        finish_last()
